import numpy as np
import ml_dtypes


def mxq(x, axis, fmt="e4m3"):
    dtype, down = {"e4m3": (ml_dtypes.float8_e4m3fn, 7), "e5m2": (ml_dtypes.float8_e5m2, 14)}[fmt]
    v = np.moveaxis(np.asarray(x, np.float32).astype(ml_dtypes.bfloat16).astype(np.float64), axis, -1)
    blocks = v.reshape(v.shape[:-1] + (-1, 32))
    amax = np.abs(blocks).max(-1, keepdims=True)
    byte = np.maximum(np.where(amax > 0, np.frexp(amax)[1] - 1 + 127, 0) - down, 1)
    scale = np.exp2(byte - 127.0)
    codes = (blocks / scale).astype(np.float32).astype(dtype).astype(np.float64)
    return np.moveaxis((codes * scale).reshape(v.shape), -1, axis)


WIDE = False


def mx_kscale(k):
    if not WIDE:
        return np.ones(k)
    levels = np.array([10, -10, 5, -5, 0])
    a = np.random.permutation(np.resize(levels, k // 512 * 4)).reshape(k // 512, 4)
    idx = np.arange(k)
    return np.exp2(a[idx // 512, idx % 128 // 32])


BF16 = ml_dtypes.bfloat16


def bf(x):
    return np.asarray(x, np.float32).astype(BF16)


def f64(x):
    return np.asarray(x).astype(np.float64)


E2M1 = np.array([0.0, 0.5, 1.0, 1.5, 2.0, 3.0, 4.0, 6.0, -0.0, -0.5, -1.0, -1.5, -2.0, -3.0, -4.0, -6.0])


def pack_weight(w, fmt):
    k, n = w.shape
    w = f64(bf(w)).reshape(k // 32, 32, n)
    amax = np.abs(w).max(1)
    if fmt == "e4m3":
        byte = np.frexp(amax)[1] - 1 + 127 - 7
    else:
        mant, ex = np.frexp(amax / 6.0)
        byte = np.where(mant > 0.5, ex, ex - 1) + 127
    byte = np.clip(np.where(amax > 0, byte, 1), 1, 254)
    scaled = (w * np.exp2(127.0 - byte)[:, None, :]).reshape(k, n).astype(np.float32)
    by_word = np.ascontiguousarray(scaled.reshape(k // 512, 128, 4, n).transpose(0, 1, 3, 2))
    if fmt == "e4m3":
        words = by_word.astype(ml_dtypes.float8_e4m3fn).view(np.uint8)
    else:
        c = by_word.astype(ml_dtypes.float4_e2m1fn).view(np.uint8) & 0xF
        words = c[..., 0::2] | (c[..., 1::2] << 4)
    return np.ascontiguousarray(words), np.ascontiguousarray(byte.astype(np.uint8).reshape(k // 512, 16, n))


def unpack_weight(words, scales, fmt):
    g, p, n, _ = words.shape
    if fmt == "e4m3":
        vals = np.ascontiguousarray(words).view(ml_dtypes.float8_e4m3fn).astype(np.float64)
    else:
        nib = np.empty((g, p, n, 4), np.uint8)
        nib[..., 0::2] = words & 0xF
        nib[..., 1::2] = words >> 4
        vals = E2M1[nib]
    vals = vals * np.repeat(np.exp2(scales.astype(np.float64) - 127.0), 8, axis=1)[..., None]
    return vals.transpose(0, 1, 3, 2).reshape(g * 512, n)


B, Hh, Ww, NB, BS, ORI, RI = 4, 4, 4, 4, 512, 6, 2
C = NB * BS
R = B * ORI * Hh * Ww
FMT = "e4m3"


def setup_inputs():
    s = mx_kscale(C)
    sb = s.reshape(NB, BS)
    t = mx_kscale(C).reshape(NB, BS)
    xh = bf(np.random.standard_normal((B, C, ORI, Hh, Ww, RI)) * s[None, :, None, None, None, None])
    w1 = np.random.standard_normal((RI, NB, BS, BS)) / np.sqrt(RI * BS) / sb[None, :, :, None] * t[None, :, None, :]
    w2 = np.random.standard_normal((RI, NB, BS, BS)) / np.sqrt(BS) / t[None, :, :, None]
    b1 = bf(np.random.standard_normal((RI, NB, BS)) * 0.3 * t[None, :, :])
    b2 = bf(np.random.standard_normal((RI, NB, BS)) * 0.3)
    w1_words, w1_scales = pack_weight(w1.reshape(-1, BS), FMT)
    w2_words, w2_scales = pack_weight(w2.reshape(-1, BS), FMT)
    return {
        "xh": xh,
        "w1_words": w1_words,
        "w1_scales": w1_scales,
        "w2_words": w2_words,
        "w2_scales": w2_scales,
        "b1": b1,
        "b2": b2,
    }


def reference(xh, w1_words, w1_scales, w2_words, w2_scales, b1, b2):
    x = f64(xh).transpose(5, 0, 2, 3, 4, 1).reshape(RI, R, NB, BS).transpose(0, 2, 1, 3)
    xq = mxq(x, 3, "e4m3")
    xr, xi = xq[0], xq[1]
    w1q = unpack_weight(w1_words, w1_scales, FMT).reshape(RI, NB, BS, BS)
    w2q = unpack_weight(w2_words, w2_scales, FMT).reshape(RI, NB, BS, BS)
    b1f = f64(b1)[:, :, None, :]
    b2f = f64(b2)[:, :, None, :]
    r1 = np.maximum((xr @ w1q[0]) - (xi @ w1q[1]) + b1f[0], 0.0)
    i1 = np.maximum((xr @ w1q[1]) + (xi @ w1q[0]) + b1f[1], 0.0)
    r1q = mxq(r1, 2, "e4m3")
    i1q = mxq(i1, 2, "e4m3")
    r2 = (r1q @ w2q[0]) - (i1q @ w2q[1]) + b2f[0]
    i2 = (r1q @ w2q[1]) + (i1q @ w2q[0]) + b2f[1]
    y = np.stack([r2, i2], axis=-1)
    y = y.transpose(1, 0, 2, 3).reshape(B, ORI, Hh, Ww, C, RI)
    return y.transpose(0, 4, 1, 2, 3, 5)

@@ -1,0 +1,233 @@
+from contextlib import ExitStack
+
+import concourse.mybir as mybir
+from concourse.masks import make_identity
+
+F32 = mybir.dt.float32
+BF16 = mybir.dt.bfloat16
+I32 = mybir.dt.int32
+U32 = mybir.dt.uint32
+U8 = mybir.dt.uint8
+FP8X4 = mybir.dt.float8_e4m3fn_x4
+ADD = mybir.AluOpType.add
+RELU = mybir.ActivationFunctionType.Relu
+
+P = 128
+PACK = 4
+BATCH = 4
+SPOTS = 96
+POS = BATCH * SPOTS
+POS_TILES = POS // P
+BLOCKS = 4
+BS = 512
+OUT_TILES = BS // P
+NEG_IM, RE, IM = 0, 1, 2
+PRODUCTS = (((RE, 0), (NEG_IM, 1)), ((RE, 1), (IM, 0)))
+RUNS = ((0, 256), (256, 128))
+MAX_QUANTIZE_WORDS = 1024
+
+FLOPS = 2 * 8 * BLOCKS * POS * BS * BS
+
+
+def powers_of_two(columns):
+    cuts = []
+    width = MAX_QUANTIZE_WORDS
+    while columns > 0:
+        if width <= columns:
+            cuts.append(width)
+            columns -= width
+        else:
+            width //= 2
+    return cuts
+
+
+def tile_scatteringmodule_pa_e_kernel(
+    tc, xh, w1_words, w1_scales, w2_words, w2_scales, b1, b2, out
+):
+    nc = tc.nc
+    x_rows = xh.rearrange("b c o h w r -> b c (o h w r)")
+    out_rows = out.rearrange("b c o h w r -> b c (o h w r)")
+
+    with ExitStack() as ctx:
+        keep = ctx.enter_context(tc.tile_pool(name="keep", bufs=1))
+        work = ctx.enter_context(tc.tile_pool(name="work", bufs=2))
+        sums = ctx.enter_context(tc.tile_pool(name="sums", bufs=2 * POS_TILES))
+        results = ctx.enter_context(tc.tile_pool(name="results", bufs=4))
+        psum_1 = ctx.enter_context(tc.psum_pool(name="psum_1", bufs=3))
+        psum_t = ctx.enter_context(tc.psum_pool(name="psum_t", bufs=2))
+        psum_2 = ctx.enter_context(tc.psum_pool(name="psum_2", bufs=3))
+        ctx.enter_context(tc.manual_schedule())
+
+        def load_x(n):
+            raw = keep.tile([P, BATCH, PACK * SPOTS * 2], BF16, name="x_raw%d" % n)
+            rows = x_rows[:, n * BS : (n + 1) * BS, :]
+            nc.sync.dma_start(out=raw[:], in_=rows.rearrange("b (p t) f -> p b (t f)", t=PACK))
+            return raw
+
+        def load_words(words, n, name):
+            codes = keep.tile([P, 2, BS], U32, name="%s%d" % (name, n), align_bytes=64)
+            by_word = words.rearrange("g p n t -> p g (n t)").bitcast(I32)
+            by_part = by_word.rearrange("p (r m) w -> p r m w", r=2)
+            nc.sync.dma_start(out=codes[:].bitcast(I32), in_=by_part[:, :, n, :])
+            return codes
+
+        def load_planes(scales, name):
+            planes = keep.tile([P, 2, BS], U8, name=name, align_bytes=64)
+            nc.vector.memset(planes[:].bitcast(I32), 0)
+            for part in range(2):
+                for quad in range(4):
+                    nc.sync.dma_start(
+                        out=planes[32 * quad : 32 * quad + 16, part, :].bitcast(I32),
+                        in_=scales[
+                            BLOCKS * part : BLOCKS * (part + 1), 4 * quad : 4 * quad + 4, :
+                        ].bitcast(I32),
+                    )
+            return planes
+
+        def quantise(grouped, width, codes, scales, first):
+            nc.vector.tensor_scalar_mul(
+                out=grouped[:, NEG_IM], in0=grouped[:, IM], scalar1=-1.0
+            )
+            flat = grouped[:].rearrange("p v c t -> p (v c t)")
+            for start, columns in ((width, 2 * width), (0, width)):
+                for cut in powers_of_two(columns):
+                    nc.vector.quantize_mx(
+                        out=codes[:, first + start : first + start + cut].bitcast(FP8X4),
+                        scales=scales[:, first + start : first + start + cut],
+                        in_=flat[:, PACK * start : PACK * (start + cut)],
+                    )
+                    start += cut
+
+        def quantise_x(n):
+            raw = x_raw[n][:].rearrange("p b (t q r) -> p r b q t", t=PACK, q=SPOTS, r=2)
+            grouped = work.tile([P, 3, POS, PACK], BF16, name="x_grouped", align_bytes=64)
+            for part, variant in ((0, RE), (1, IM)):
+                nc.scalar.copy(
+                    out=grouped[:, variant].rearrange("p (b q) t -> p b q t", b=BATCH),
+                    in_=raw[:, part],
+                )
+            codes = work.tile([P, 3 * POS], U32, name="x_codes", align_bytes=64)
+            scales = work.tile([P, 3 * POS], U8, name="x_scales", align_bytes=64)
+            quantise(grouped, POS, codes, scales, 0)
+            return codes, scales
+
+        def layer_1(n, x_codes, x_scales):
+            pre = []
+            for a in range(POS_TILES):
+                for part in range(2):
+                    acc = psum_1.tile([P, BS], F32, name="acc_1")
+                    for i, (variant, w_part) in enumerate(PRODUCTS[part]):
+                        cols = slice(variant * POS + a * P, variant * POS + (a + 1) * P)
+                        nc.tensor.matmul_mx(
+                            out=acc[:],
+                            lhsT=x_codes[:, cols].bitcast(FP8X4),
+                            lhsT_scale=x_scales[:, cols],
+                            rhs=w1_codes[n][:, w_part, :].bitcast(FP8X4),
+                            rhs_scale=w1_planes[4 * n : P, w_part, :],
+                            start=(i == 0),
+                            stop=(i == 1),
+                        )
+                    biased = sums.tile([P, PACK, P], BF16, name="biased")
+                    nc.vector.tensor_tensor(
+                        out=biased[:],
+                        in0=acc[:].rearrange("p (j t) -> p t j", t=PACK),
+                        in1=b1_all[:, part, n, :].rearrange("p (j t) -> p t j", t=PACK),
+                        op=ADD,
+                    )
+                    pre.append(biased)
+            return pre
+
+        def transpose_and_quantise(pre):
+            codes = work.tile([P, 3 * POS], U32, name="h_codes", align_bytes=64)
+            scales = work.tile([P, 3 * POS], U8, name="h_scales", align_bytes=64)
+            for first, width in RUNS:
+                grouped = work.tile(
+                    [P, 3, width, PACK], BF16, name="h_grouped%d" % width, align_bytes=64
+                )
+                for a in range(first // P, (first + width) // P):
+                    turned = psum_t.tile([P, 2, PACK, P], BF16, name="turned")
+                    for part in range(2):
+                        for t in range(PACK):
+                            nc.tensor.transpose(
+                                out=turned[:, part, t, :],
+                                in_=pre[2 * a + part][:, t, :],
+                                identity=identity[:],
+                            )
+                    nc.scalar.activation(
+                        out=grouped[:, RE : IM + 1, a * P - first : (a + 1) * P - first, :],
+                        in_=turned[:].rearrange("p r t c -> p r c t"),
+                        func=RELU,
+                    )
+                quantise(grouped, width, codes, scales, 3 * first)
+            return codes, scales
+
+        def layer_2(n, h_codes, h_scales):
+            for m in range(OUT_TILES):
+                result = results.tile([P, POS, 2], F32, name="result")
+                for first, width in RUNS:
+                    acc = psum_2.tile([P, 2, width], F32, name="acc_2_%d" % width, tag="acc_2")
+                    for w_part, start in ((0, width), (1, 0)):
+                        cols = slice(3 * first + start, 3 * first + start + 2 * width)
+                        nc.tensor.matmul_mx(
+                            out=acc[:].rearrange("p r c -> p (r c)"),
+                            lhsT=w2_codes[n][:, w_part, m * P : (m + 1) * P].bitcast(FP8X4),
+                            lhsT_scale=w2_planes[4 * n : P, w_part, m * P : (m + 1) * P],
+                            rhs=h_codes[:, cols].bitcast(FP8X4),
+                            rhs_scale=h_scales[:, cols],
+                            start=(w_part == 0),
+                            stop=(w_part == 1),
+                        )
+                    nc.vector.tensor_tensor(
+                        out=result[:, first : first + width, :],
+                        in0=acc[:].rearrange("p r c -> p c r"),
+                        in1=b2_cols[:, n * OUT_TILES + m, :]
+                        .unsqueeze(1)
+                        .to_broadcast([P, width, 2]),
+                        op=ADD,
+                    )
+                channel = n * BS + m * P
+                nc.sync.dma_start(
+                    out=out_rows[:, channel : channel + P, :].rearrange("b c f -> c b f"),
+                    in_=result[:].rearrange("p (b q) r -> p b (q r)", b=BATCH),
+                )
+
+        x_raw = [load_x(0)]
+        b2_rows = keep.tile([P, P], BF16, name="b2_rows")
+        nc.vector.memset(b2_rows[:], 0.0)
+        nc.sync.dma_start(
+            out=b2_rows[0 : 2 * BLOCKS * OUT_TILES, :],
+            in_=b2.rearrange("r n (m j) -> (r n m) j", j=P),
+        )
+        w1_planes = load_planes(w1_scales, "w1_planes")
+        w1_codes = [load_words(w1_words, 0, "w1_codes")]
+        b1_all = keep.tile([P, 2, BLOCKS, BS], BF16, name="b1_all")
+        nc.sync.dma_start(
+            out=b1_all[:].rearrange("p r n k -> p (r n k)"),
+            in_=b1.rearrange("r n k -> (r n k)").partition_broadcast(P),
+        )
+        w2_planes = load_planes(w2_scales, "w2_planes")
+        w2_codes = [load_words(w2_words, 0, "w2_codes")]
+        for n in range(1, BLOCKS):
+            x_raw.append(load_x(n))
+            w1_codes.append(load_words(w1_words, n, "w1_codes"))
+            w2_codes.append(load_words(w2_words, n, "w2_codes"))
+
+        identity = keep.tile([P, P], BF16, name="identity")
+        make_identity(nc, identity[:])
+        b2_turned = psum_t.tile([P, P], BF16, name="b2_turned", tag="turned")
+        nc.tensor.transpose(out=b2_turned[:], in_=b2_rows[:], identity=identity[:])
+        b2_cols = keep.tile([P, BLOCKS * OUT_TILES, 2], F32, name="b2_cols")
+        nc.vector.tensor_copy(
+            out=b2_cols[:],
+            in_=b2_turned[:, 0 : 2 * BLOCKS * OUT_TILES].rearrange("p (r g) -> p g r", r=2),
+        )
+
+        x_mx = quantise_x(0)
+        pre = layer_1(0, x_mx[0], x_mx[1])
+        for n in range(BLOCKS):
+            if n + 1 < BLOCKS:
+                x_mx = quantise_x(n + 1)
+            h_mx = transpose_and_quantise(pre)
+            if n + 1 < BLOCKS:
+                pre = layer_1(n + 1, x_mx[0], x_mx[1])
+            layer_2(n, h_mx[0], h_mx[1])

@@ -72,16 +72,13 @@ def tile_scatteringmodule_pa_e_kernel(
             return codes
 
         def load_planes(scales, name):
-            planes = keep.tile([P, 2, BS], U8, name=name, align_bytes=64)
+            planes = keep.tile([P, 2 * BLOCKS, BS], U8, name=name, align_bytes=64)
             nc.vector.memset(planes[:].bitcast(I32), 0)
-            for part in range(2):
-                for quad in range(4):
-                    nc.sync.dma_start(
-                        out=planes[32 * quad : 32 * quad + 16, part, :].bitcast(I32),
-                        in_=scales[
-                            BLOCKS * part : BLOCKS * (part + 1), 4 * quad : 4 * quad + 4, :
-                        ].bitcast(I32),
-                    )
+            by_row = scales.rearrange("e (q r) c -> r q e c", r=4)
+            for r in range(4):
+                nc.sync.dma_start(
+                    out=planes[r:P:32, :, :].bitcast(I32), in_=by_row[r].bitcast(I32)
+                )
             return planes
 
         def quantise(grouped, width, codes, scales, first):
@@ -98,14 +95,29 @@ def tile_scatteringmodule_pa_e_kernel(
                     )
                     start += cut
 
-        def quantise_x(n):
+        def prepare(n, copy_imaginary):
+            spread = psum_t.tile([P, 2, BS], BF16, name="spread", tag="turned")
+            for part in range(2):
+                g = part * BLOCKS + n
+                nc.tensor.matmul(
+                    out=spread[:, part, :],
+                    lhsT=identity[:, g : g + 1].to_broadcast([P, P]),
+                    rhs=b1_rows[:],
+                    start=True,
+                    stop=True,
+                )
             raw = x_raw[n][:].rearrange("p b (t q r) -> p r b q t", t=PACK, q=SPOTS, r=2)
             grouped = work.tile([P, 3, POS, PACK], BF16, name="x_grouped", align_bytes=64)
-            for part, variant in ((0, RE), (1, IM)):
-                nc.scalar.copy(
-                    out=grouped[:, variant].rearrange("p (b q) t -> p b q t", b=BATCH),
-                    in_=raw[:, part],
-                )
+            nc.scalar.copy(
+                out=grouped[:, RE].rearrange("p (b q) t -> p b q t", b=BATCH), in_=raw[:, 0]
+            )
+            copy_imaginary(
+                out=grouped[:, IM].rearrange("p (b q) t -> p b q t", b=BATCH), in_=raw[:, 1]
+            )
+            nc.scalar.copy(out=b1_all[:, n], in_=spread[:])
+            return grouped
+
+        def quantise_x(grouped):
             codes = work.tile([P, 3 * POS], U32, name="x_codes", align_bytes=64)
             scales = work.tile([P, 3 * POS], U8, name="x_scales", align_bytes=64)
             quantise(grouped, POS, codes, scales, 0)
@@ -115,7 +127,7 @@ def tile_scatteringmodule_pa_e_kernel(
             pre = []
             for a in range(POS_TILES):
                 for part in range(2):
-                    acc = psum_1.tile([P, BS], F32, name="acc_1")
+                    acc = psum_1.tile([P, BS], F32, name="acc_1", tag="acc_1")
                     for i, (variant, w_part) in enumerate(PRODUCTS[part]):
                         cols = slice(variant * POS + a * P, variant * POS + (a + 1) * P)
                         nc.tensor.matmul_mx(
@@ -123,7 +135,7 @@ def tile_scatteringmodule_pa_e_kernel(
                             lhsT=x_codes[:, cols].bitcast(FP8X4),
                             lhsT_scale=x_scales[:, cols],
                             rhs=w1_codes[n][:, w_part, :].bitcast(FP8X4),
-                            rhs_scale=w1_planes[4 * n : P, w_part, :],
+                            rhs_scale=w1_planes[:, w_part * BLOCKS + n, :],
                             start=(i == 0),
                             stop=(i == 1),
                         )
@@ -131,15 +143,14 @@ def tile_scatteringmodule_pa_e_kernel(
                     nc.vector.tensor_tensor(
                         out=biased[:],
                         in0=acc[:].rearrange("p (j t) -> p t j", t=PACK),
-                        in1=b1_all[:, part, n, :].rearrange("p (j t) -> p t j", t=PACK),
+                        in1=b1_all[:, n, part, :].rearrange("p (j t) -> p t j", t=PACK),
                         op=ADD,
                     )
                     pre.append(biased)
             return pre
 
-        def transpose_and_quantise(pre):
-            codes = work.tile([P, 3 * POS], U32, name="h_codes", align_bytes=64)
-            scales = work.tile([P, 3 * POS], U8, name="h_scales", align_bytes=64)
+        def transpose(pre):
+            runs = []
             for first, width in RUNS:
                 grouped = work.tile(
                     [P, 3, width, PACK], BF16, name="h_grouped%d" % width, align_bytes=64
@@ -158,6 +169,13 @@ def tile_scatteringmodule_pa_e_kernel(
                         in_=turned[:].rearrange("p r t c -> p r c t"),
                         func=RELU,
                     )
+                runs.append(grouped)
+            return runs
+
+        def quantise_h(runs):
+            codes = work.tile([P, 3 * POS], U32, name="h_codes", align_bytes=64)
+            scales = work.tile([P, 3 * POS], U8, name="h_scales", align_bytes=64)
+            for (first, width), grouped in zip(RUNS, runs):
                 quantise(grouped, width, codes, scales, 3 * first)
             return codes, scales
 
@@ -171,7 +189,7 @@ def tile_scatteringmodule_pa_e_kernel(
                         nc.tensor.matmul_mx(
                             out=acc[:].rearrange("p r c -> p (r c)"),
                             lhsT=w2_codes[n][:, w_part, m * P : (m + 1) * P].bitcast(FP8X4),
-                            lhsT_scale=w2_planes[4 * n : P, w_part, m * P : (m + 1) * P],
+                            lhsT_scale=w2_planes[:, w_part * BLOCKS + n, m * P : (m + 1) * P],
                             rhs=h_codes[:, cols].bitcast(FP8X4),
                             rhs_scale=h_scales[:, cols],
                             start=(w_part == 0),
@@ -191,29 +209,32 @@ def tile_scatteringmodule_pa_e_kernel(
                     in_=result[:].rearrange("p (b q) r -> p b (q r)", b=BATCH),
                 )
 
-        x_raw = [load_x(0)]
+        b1_rows = keep.tile([P, BS], BF16, name="b1_rows")
+        nc.vector.memset(b1_rows[:], 0.0)
         b2_rows = keep.tile([P, P], BF16, name="b2_rows")
         nc.vector.memset(b2_rows[:], 0.0)
-        nc.sync.dma_start(
-            out=b2_rows[0 : 2 * BLOCKS * OUT_TILES, :],
-            in_=b2.rearrange("r n (m j) -> (r n m) j", j=P),
-        )
+        x_raw = [load_x(0)]
+        nc.scalar.dma_start(out=b1_rows[0 : 2 * BLOCKS, :], in_=b1.rearrange("r n k -> (r n) k"))
         w1_planes = load_planes(w1_scales, "w1_planes")
         w1_codes = [load_words(w1_words, 0, "w1_codes")]
-        b1_all = keep.tile([P, 2, BLOCKS, BS], BF16, name="b1_all")
-        nc.sync.dma_start(
-            out=b1_all[:].rearrange("p r n k -> p (r n k)"),
-            in_=b1.rearrange("r n k -> (r n k)").partition_broadcast(P),
+        x_raw.append(load_x(1))
+        nc.scalar.dma_start(
+            out=b2_rows[0 : 2 * BLOCKS * OUT_TILES, :],
+            in_=b2.rearrange("r n (m j) -> (r n m) j", j=P),
         )
         w2_planes = load_planes(w2_scales, "w2_planes")
         w2_codes = [load_words(w2_words, 0, "w2_codes")]
         for n in range(1, BLOCKS):
-            x_raw.append(load_x(n))
             w1_codes.append(load_words(w1_words, n, "w1_codes"))
+            if n + 1 < BLOCKS:
+                x_raw.append(load_x(n + 1))
             w2_codes.append(load_words(w2_words, n, "w2_codes"))
 
         identity = keep.tile([P, P], BF16, name="identity")
         make_identity(nc, identity[:])
+
+        b1_all = keep.tile([P, BLOCKS, 2, BS], BF16, name="b1_all")
+
         b2_turned = psum_t.tile([P, P], BF16, name="b2_turned", tag="turned")
         nc.tensor.transpose(out=b2_turned[:], in_=b2_rows[:], identity=identity[:])
         b2_cols = keep.tile([P, BLOCKS * OUT_TILES, 2], F32, name="b2_cols")
@@ -222,12 +243,19 @@ def tile_scatteringmodule_pa_e_kernel(
             in_=b2_turned[:, 0 : 2 * BLOCKS * OUT_TILES].rearrange("p (r g) -> p g r", r=2),
         )
 
-        x_mx = quantise_x(0)
+        x_grouped = [prepare(0, nc.vector.tensor_copy), prepare(1, nc.scalar.copy)]
+        x_mx = quantise_x(x_grouped[0])
         pre = layer_1(0, x_mx[0], x_mx[1])
+        h_mx = None
         for n in range(BLOCKS):
+            runs = transpose(pre)
+            if n + 2 < BLOCKS:
+                x_grouped.append(prepare(n + 2, nc.scalar.copy))
             if n + 1 < BLOCKS:
-                x_mx = quantise_x(n + 1)
-            h_mx = transpose_and_quantise(pre)
+                x_mx = quantise_x(x_grouped[n + 1])
+            if n > 0:
+                layer_2(n - 1, h_mx[0], h_mx[1])
+            h_mx = quantise_h(runs)
             if n + 1 < BLOCKS:
                 pre = layer_1(n + 1, x_mx[0], x_mx[1])
-            layer_2(n, h_mx[0], h_mx[1])
+        layer_2(BLOCKS - 1, h_mx[0], h_mx[1])

@@ -10,6 +10,7 @@ U32 = mybir.dt.uint32
 U8 = mybir.dt.uint8
 FP8X4 = mybir.dt.float8_e4m3fn_x4
 ADD = mybir.AluOpType.add
+MULT = mybir.AluOpType.mult
 RELU = mybir.ActivationFunctionType.Relu
 
 P = 128
@@ -53,9 +54,8 @@ def tile_scatteringmodule_pa_e_kernel(
         work = ctx.enter_context(tc.tile_pool(name="work", bufs=2))
         sums = ctx.enter_context(tc.tile_pool(name="sums", bufs=2 * POS_TILES))
         results = ctx.enter_context(tc.tile_pool(name="results", bufs=4))
-        psum_1 = ctx.enter_context(tc.psum_pool(name="psum_1", bufs=3))
+        psum_mx = ctx.enter_context(tc.psum_pool(name="psum_mx", bufs=6))
         psum_t = ctx.enter_context(tc.psum_pool(name="psum_t", bufs=2))
-        psum_2 = ctx.enter_context(tc.psum_pool(name="psum_2", bufs=3))
         ctx.enter_context(tc.manual_schedule())
 
         def load_x(n):
@@ -82,9 +82,6 @@ def tile_scatteringmodule_pa_e_kernel(
             return planes
 
         def quantise(grouped, width, codes, scales, first):
-            nc.vector.tensor_scalar_mul(
-                out=grouped[:, NEG_IM], in0=grouped[:, IM], scalar1=-1.0
-            )
             flat = grouped[:].rearrange("p v c t -> p (v c t)")
             for start, columns in ((width, 2 * width), (0, width)):
                 for cut in powers_of_two(columns):
@@ -95,7 +92,7 @@ def tile_scatteringmodule_pa_e_kernel(
                     )
                     start += cut
 
-        def prepare(n, copy_imaginary):
+        def prepare(n):
             spread = psum_t.tile([P, 2, BS], BF16, name="spread", tag="turned")
             for part in range(2):
                 g = part * BLOCKS + n
@@ -108,12 +105,24 @@ def tile_scatteringmodule_pa_e_kernel(
                 )
             raw = x_raw[n][:].rearrange("p b (t q r) -> p r b q t", t=PACK, q=SPOTS, r=2)
             grouped = work.tile([P, 3, POS, PACK], BF16, name="x_grouped", align_bytes=64)
-            nc.scalar.copy(
-                out=grouped[:, RE].rearrange("p (b q) t -> p b q t", b=BATCH), in_=raw[:, 0]
-            )
-            copy_imaginary(
-                out=grouped[:, IM].rearrange("p (b q) t -> p b q t", b=BATCH), in_=raw[:, 1]
-            )
+            by_batch = grouped[:].rearrange("p v (b q) t -> p v b q t", b=BATCH)
+            nc.scalar.copy(out=by_batch[:, RE], in_=raw[:, 0])
+            if n == 0:
+                nc.vector.tensor_copy(out=by_batch[:, IM], in_=raw[:, 1])
+                nc.vector.tensor_scalar_mul(
+                    out=grouped[:, NEG_IM], in0=grouped[:, IM], scalar1=-1.0
+                )
+            else:
+                for b in range(BATCH):
+                    for variant, sign in ((IM, 1.0), (NEG_IM, -1.0)):
+                        nc.gpsimd.tensor_scalar(
+                            out=by_batch[:, variant, b],
+                            in0=raw[:, 1, b],
+                            scalar1=sign,
+                            scalar2=0.0,
+                            op0=MULT,
+                            op1=ADD,
+                        )
             nc.scalar.copy(out=b1_all[:, n], in_=spread[:])
             return grouped
 
@@ -127,7 +136,7 @@ def tile_scatteringmodule_pa_e_kernel(
             pre = []
             for a in range(POS_TILES):
                 for part in range(2):
-                    acc = psum_1.tile([P, BS], F32, name="acc_1", tag="acc_1")
+                    acc = psum_mx.tile([P, BS], F32, name="acc_1", tag="acc")
                     for i, (variant, w_part) in enumerate(PRODUCTS[part]):
                         cols = slice(variant * POS + a * P, variant * POS + (a + 1) * P)
                         nc.tensor.matmul_mx(
@@ -170,6 +179,8 @@ def tile_scatteringmodule_pa_e_kernel(
                         func=RELU,
                     )
                 runs.append(grouped)
+            for grouped in runs:
+                nc.scalar.mul(out=grouped[:, NEG_IM], in_=grouped[:, IM], mul=-1.0)
             return runs
 
         def quantise_h(runs):
@@ -183,7 +194,7 @@ def tile_scatteringmodule_pa_e_kernel(
             for m in range(OUT_TILES):
                 result = results.tile([P, POS, 2], F32, name="result")
                 for first, width in RUNS:
-                    acc = psum_2.tile([P, 2, width], F32, name="acc_2_%d" % width, tag="acc_2")
+                    acc = psum_mx.tile([P, 2, width], F32, name="acc_2_%d" % width, tag="acc")
                     for w_part, start in ((0, width), (1, 0)):
                         cols = slice(3 * first + start, 3 * first + start + 2 * width)
                         nc.tensor.matmul_mx(
@@ -243,14 +254,14 @@ def tile_scatteringmodule_pa_e_kernel(
             in_=b2_turned[:, 0 : 2 * BLOCKS * OUT_TILES].rearrange("p (r g) -> p g r", r=2),
         )
 
-        x_grouped = [prepare(0, nc.vector.tensor_copy), prepare(1, nc.scalar.copy)]
+        x_grouped = [prepare(0), prepare(1)]
         x_mx = quantise_x(x_grouped[0])
         pre = layer_1(0, x_mx[0], x_mx[1])
         h_mx = None
         for n in range(BLOCKS):
             runs = transpose(pre)
             if n + 2 < BLOCKS:
-                x_grouped.append(prepare(n + 2, nc.scalar.copy))
+                x_grouped.append(prepare(n + 2))
             if n + 1 < BLOCKS:
                 x_mx = quantise_x(x_grouped[n + 1])
             if n > 0:

@@ -123,7 +123,10 @@ def tile_scatteringmodule_pa_e_kernel(
                             op0=MULT,
                             op1=ADD,
                         )
-            nc.scalar.copy(out=b1_all[:, n], in_=spread[:])
+            nc.scalar.copy(
+                out=b1_all[:, n].rearrange("p r (t j) -> p r t j", t=PACK),
+                in_=spread[:].rearrange("p r (j t) -> p r t j", t=PACK),
+            )
             return grouped
 
         def quantise_x(grouped):
@@ -152,7 +155,7 @@ def tile_scatteringmodule_pa_e_kernel(
                     nc.vector.tensor_tensor(
                         out=biased[:],
                         in0=acc[:].rearrange("p (j t) -> p t j", t=PACK),
-                        in1=b1_all[:, n, part, :].rearrange("p (j t) -> p t j", t=PACK),
+                        in1=b1_all[:, n, part, :].rearrange("p (t j) -> p t j", t=PACK),
                         op=ADD,
                     )
                     pre.append(biased)

@@ -26,6 +26,8 @@ NEG_IM, RE, IM = 0, 1, 2
 PRODUCTS = (((RE, 0), (NEG_IM, 1)), ((RE, 1), (IM, 0)))
 RUNS = ((0, 256), (256, 128))
 MAX_QUANTIZE_WORDS = 1024
+MX_BANKS = 6
+EARLY_TILES = MX_BANKS // len(RUNS)
 
 FLOPS = 2 * 8 * BLOCKS * POS * BS * BS
 
@@ -54,7 +56,7 @@ def tile_scatteringmodule_pa_e_kernel(
         work = ctx.enter_context(tc.tile_pool(name="work", bufs=2))
         sums = ctx.enter_context(tc.tile_pool(name="sums", bufs=2 * POS_TILES))
         results = ctx.enter_context(tc.tile_pool(name="results", bufs=4))
-        psum_mx = ctx.enter_context(tc.psum_pool(name="psum_mx", bufs=6))
+        psum_mx = ctx.enter_context(tc.psum_pool(name="psum_mx", bufs=MX_BANKS))
         psum_t = ctx.enter_context(tc.psum_pool(name="psum_t", bufs=2))
         ctx.enter_context(tc.manual_schedule())
 
@@ -123,10 +125,7 @@ def tile_scatteringmodule_pa_e_kernel(
                             op0=MULT,
                             op1=ADD,
                         )
-            nc.scalar.copy(
-                out=b1_all[:, n].rearrange("p r (t j) -> p r t j", t=PACK),
-                in_=spread[:].rearrange("p r (j t) -> p r t j", t=PACK),
-            )
+            nc.scalar.copy(out=b1_all[:, n], in_=spread[:])
             return grouped
 
         def quantise_x(grouped):
@@ -155,7 +154,7 @@ def tile_scatteringmodule_pa_e_kernel(
                     nc.vector.tensor_tensor(
                         out=biased[:],
                         in0=acc[:].rearrange("p (j t) -> p t j", t=PACK),
-                        in1=b1_all[:, n, part, :].rearrange("p (t j) -> p t j", t=PACK),
+                        in1=b1_all[:, n, part, :].rearrange("p (j t) -> p t j", t=PACK),
                         op=ADD,
                     )
                     pre.append(biased)
@@ -183,7 +182,14 @@ def tile_scatteringmodule_pa_e_kernel(
                     )
                 runs.append(grouped)
             for grouped in runs:
-                nc.scalar.mul(out=grouped[:, NEG_IM], in_=grouped[:, IM], mul=-1.0)
+                nc.gpsimd.tensor_scalar(
+                    out=grouped[:, NEG_IM],
+                    in0=grouped[:, IM],
+                    scalar1=-1.0,
+                    scalar2=0.0,
+                    op0=MULT,
+                    op1=ADD,
+                )
             return runs
 
         def quantise_h(runs):
@@ -193,8 +199,8 @@ def tile_scatteringmodule_pa_e_kernel(
                 quantise(grouped, width, codes, scales, 3 * first)
             return codes, scales
 
-        def layer_2(n, h_codes, h_scales):
-            for m in range(OUT_TILES):
+        def layer_2(n, h_codes, h_scales, tiles):
+            for m in tiles:
                 result = results.tile([P, POS, 2], F32, name="result")
                 for first, width in RUNS:
                     acc = psum_mx.tile([P, 2, width], F32, name="acc_2_%d" % width, tag="acc")
@@ -259,17 +265,17 @@ def tile_scatteringmodule_pa_e_kernel(
 
         x_grouped = [prepare(0), prepare(1)]
         x_mx = quantise_x(x_grouped[0])
-        pre = layer_1(0, x_mx[0], x_mx[1])
         h_mx = None
         for n in range(BLOCKS):
-            runs = transpose(pre)
-            if n + 2 < BLOCKS:
-                x_grouped.append(prepare(n + 2))
+            pre = layer_1(n, x_mx[0], x_mx[1])
             if n + 1 < BLOCKS:
                 x_mx = quantise_x(x_grouped[n + 1])
             if n > 0:
-                layer_2(n - 1, h_mx[0], h_mx[1])
+                layer_2(n - 1, h_mx[0], h_mx[1], range(EARLY_TILES))
+            runs = transpose(pre)
+            if n > 0:
+                layer_2(n - 1, h_mx[0], h_mx[1], range(EARLY_TILES, OUT_TILES))
+            if n + 2 < BLOCKS:
+                x_grouped.append(prepare(n + 2))
             h_mx = quantise_h(runs)
-            if n + 1 < BLOCKS:
-                pre = layer_1(n + 1, x_mx[0], x_mx[1])
-        layer_2(BLOCKS - 1, h_mx[0], h_mx[1])
+        layer_2(BLOCKS - 1, h_mx[0], h_mx[1], range(OUT_TILES))

@@ -26,8 +26,6 @@ NEG_IM, RE, IM = 0, 1, 2
 PRODUCTS = (((RE, 0), (NEG_IM, 1)), ((RE, 1), (IM, 0)))
 RUNS = ((0, 256), (256, 128))
 MAX_QUANTIZE_WORDS = 1024
-MX_BANKS = 6
-EARLY_TILES = MX_BANKS // len(RUNS)
 
 FLOPS = 2 * 8 * BLOCKS * POS * BS * BS
 
@@ -56,7 +54,7 @@ def tile_scatteringmodule_pa_e_kernel(
         work = ctx.enter_context(tc.tile_pool(name="work", bufs=2))
         sums = ctx.enter_context(tc.tile_pool(name="sums", bufs=2 * POS_TILES))
         results = ctx.enter_context(tc.tile_pool(name="results", bufs=4))
-        psum_mx = ctx.enter_context(tc.psum_pool(name="psum_mx", bufs=MX_BANKS))
+        psum_mx = ctx.enter_context(tc.psum_pool(name="psum_mx", bufs=6))
         psum_t = ctx.enter_context(tc.psum_pool(name="psum_t", bufs=2))
         ctx.enter_context(tc.manual_schedule())
 
@@ -150,12 +148,9 @@ def tile_scatteringmodule_pa_e_kernel(
                             start=(i == 0),
                             stop=(i == 1),
                         )
-                    biased = sums.tile([P, PACK, P], BF16, name="biased")
+                    biased = sums.tile([P, BS], BF16, name="biased")
                     nc.vector.tensor_tensor(
-                        out=biased[:],
-                        in0=acc[:].rearrange("p (j t) -> p t j", t=PACK),
-                        in1=b1_all[:, n, part, :].rearrange("p (j t) -> p t j", t=PACK),
-                        op=ADD,
+                        out=biased[:], in0=acc[:], in1=b1_all[:, n, part, :], op=ADD
                     )
                     pre.append(biased)
             return pre
@@ -172,7 +167,7 @@ def tile_scatteringmodule_pa_e_kernel(
                         for t in range(PACK):
                             nc.tensor.transpose(
                                 out=turned[:, part, t, :],
-                                in_=pre[2 * a + part][:, t, :],
+                                in_=pre[2 * a + part][:, t:BS:PACK],
                                 identity=identity[:],
                             )
                     nc.scalar.activation(
@@ -182,14 +177,7 @@ def tile_scatteringmodule_pa_e_kernel(
                     )
                 runs.append(grouped)
             for grouped in runs:
-                nc.gpsimd.tensor_scalar(
-                    out=grouped[:, NEG_IM],
-                    in0=grouped[:, IM],
-                    scalar1=-1.0,
-                    scalar2=0.0,
-                    op0=MULT,
-                    op1=ADD,
-                )
+                nc.scalar.mul(out=grouped[:, NEG_IM], in_=grouped[:, IM], mul=-1.0)
             return runs
 
         def quantise_h(runs):
@@ -199,8 +187,8 @@ def tile_scatteringmodule_pa_e_kernel(
                 quantise(grouped, width, codes, scales, 3 * first)
             return codes, scales
 
-        def layer_2(n, h_codes, h_scales, tiles):
-            for m in tiles:
+        def layer_2(n, h_codes, h_scales):
+            for m in range(OUT_TILES):
                 result = results.tile([P, POS, 2], F32, name="result")
                 for first, width in RUNS:
                     acc = psum_mx.tile([P, 2, width], F32, name="acc_2_%d" % width, tag="acc")
@@ -265,17 +253,17 @@ def tile_scatteringmodule_pa_e_kernel(
 
         x_grouped = [prepare(0), prepare(1)]
         x_mx = quantise_x(x_grouped[0])
+        pre = layer_1(0, x_mx[0], x_mx[1])
         h_mx = None
         for n in range(BLOCKS):
-            pre = layer_1(n, x_mx[0], x_mx[1])
+            runs = transpose(pre)
+            if n + 2 < BLOCKS:
+                x_grouped.append(prepare(n + 2))
             if n + 1 < BLOCKS:
                 x_mx = quantise_x(x_grouped[n + 1])
             if n > 0:
-                layer_2(n - 1, h_mx[0], h_mx[1], range(EARLY_TILES))
-            runs = transpose(pre)
-            if n > 0:
-                layer_2(n - 1, h_mx[0], h_mx[1], range(EARLY_TILES, OUT_TILES))
-            if n + 2 < BLOCKS:
-                x_grouped.append(prepare(n + 2))
+                layer_2(n - 1, h_mx[0], h_mx[1])
             h_mx = quantise_h(runs)
-        layer_2(BLOCKS - 1, h_mx[0], h_mx[1], range(OUT_TILES))
+            if n + 1 < BLOCKS:
+                pre = layer_1(n + 1, x_mx[0], x_mx[1])
+        layer_2(BLOCKS - 1, h_mx[0], h_mx[1])

@@ -56,7 +56,6 @@ def tile_scatteringmodule_pa_e_kernel(
         results = ctx.enter_context(tc.tile_pool(name="results", bufs=4))
         psum_mx = ctx.enter_context(tc.psum_pool(name="psum_mx", bufs=6))
         psum_t = ctx.enter_context(tc.psum_pool(name="psum_t", bufs=2))
-        ctx.enter_context(tc.manual_schedule())
 
         def load_x(n):
             raw = keep.tile([P, BATCH, PACK * SPOTS * 2], BF16, name="x_raw%d" % n)
@@ -148,9 +147,12 @@ def tile_scatteringmodule_pa_e_kernel(
                             start=(i == 0),
                             stop=(i == 1),
                         )
-                    biased = sums.tile([P, BS], BF16, name="biased")
+                    biased = sums.tile([P, PACK, P], BF16, name="biased")
                     nc.vector.tensor_tensor(
-                        out=biased[:], in0=acc[:], in1=b1_all[:, n, part, :], op=ADD
+                        out=biased[:],
+                        in0=acc[:].rearrange("p (j t) -> p t j", t=PACK),
+                        in1=b1_all[:, n, part, :].rearrange("p (j t) -> p t j", t=PACK),
+                        op=ADD,
                     )
                     pre.append(biased)
             return pre
@@ -167,7 +169,7 @@ def tile_scatteringmodule_pa_e_kernel(
                         for t in range(PACK):
                             nc.tensor.transpose(
                                 out=turned[:, part, t, :],
-                                in_=pre[2 * a + part][:, t:BS:PACK],
+                                in_=pre[2 * a + part][:, t, :],
                                 identity=identity[:],
                             )
                     nc.scalar.activation(

@@ -18,13 +18,11 @@ PACK = 4
 BATCH = 4
 SPOTS = 96
 POS = BATCH * SPOTS
-POS_TILES = POS // P
 BLOCKS = 4
 BS = 512
 OUT_TILES = BS // P
 NEG_IM, RE, IM = 0, 1, 2
-PRODUCTS = (((RE, 0), (NEG_IM, 1)), ((RE, 1), (IM, 0)))
-RUNS = ((0, 256), (256, 128))
+RUNS = ((0, 64), (64, 32))
 MAX_QUANTIZE_WORDS = 1024
 
 FLOPS = 2 * 8 * BLOCKS * POS * BS * BS
@@ -52,10 +50,8 @@ def tile_scatteringmodule_pa_e_kernel(
     with ExitStack() as ctx:
         keep = ctx.enter_context(tc.tile_pool(name="keep", bufs=1))
         work = ctx.enter_context(tc.tile_pool(name="work", bufs=2))
-        sums = ctx.enter_context(tc.tile_pool(name="sums", bufs=2 * POS_TILES))
         results = ctx.enter_context(tc.tile_pool(name="results", bufs=4))
-        psum_mx = ctx.enter_context(tc.psum_pool(name="psum_mx", bufs=6))
-        psum_t = ctx.enter_context(tc.psum_pool(name="psum_t", bufs=2))
+        psum = ctx.enter_context(tc.psum_pool(name="psum", bufs=8))
 
         def load_x(n):
             raw = keep.tile([P, BATCH, PACK * SPOTS * 2], BF16, name="x_raw%d" % n)
@@ -71,13 +67,16 @@ def tile_scatteringmodule_pa_e_kernel(
             return codes
 
         def load_planes(scales, name):
-            planes = keep.tile([P, 2 * BLOCKS, BS], U8, name=name, align_bytes=64)
+            planes = keep.tile([P, 2, BS], U8, name=name, align_bytes=64)
             nc.vector.memset(planes[:].bitcast(I32), 0)
-            by_row = scales.rearrange("e (q r) c -> r q e c", r=4)
-            for r in range(4):
-                nc.sync.dma_start(
-                    out=planes[r:P:32, :, :].bitcast(I32), in_=by_row[r].bitcast(I32)
-                )
+            for quad in range(4):
+                for part in range(2):
+                    nc.sync.dma_start(
+                        out=planes[32 * quad : 32 * quad + 16, part, :].bitcast(I32),
+                        in_=scales[
+                            part * BLOCKS : (part + 1) * BLOCKS, 4 * quad : 4 * quad + 4, :
+                        ].bitcast(I32),
+                    )
             return planes
 
         def quantise(grouped, width, codes, scales, first):
@@ -91,142 +90,127 @@ def tile_scatteringmodule_pa_e_kernel(
                     )
                     start += cut
 
-        def prepare(n):
-            spread = psum_t.tile([P, 2, BS], BF16, name="spread", tag="turned")
-            for part in range(2):
-                g = part * BLOCKS + n
-                nc.tensor.matmul(
-                    out=spread[:, part, :],
-                    lhsT=identity[:, g : g + 1].to_broadcast([P, P]),
-                    rhs=b1_rows[:],
-                    start=True,
-                    stop=True,
-                )
+        def quantise_runs(runs, name):
+            codes = work.tile([P, 3 * POS], U32, name=name + "_codes", align_bytes=64)
+            scales = work.tile([P, 3 * POS], U8, name=name + "_scales", align_bytes=64)
+            for (q0, qn), grouped in zip(RUNS, runs):
+                quantise(grouped, BATCH * qn, codes, scales, 3 * BATCH * q0)
+            return codes, scales
+
+        def permute_w1(n):
+            codes = keep.tile([P, 2, BS], U32, name="w1_codes%d" % n, align_bytes=64)
+            nc.vector.tensor_copy(
+                out=codes[:].bitcast(I32).rearrange("p r (t m) -> p r t m", t=PACK),
+                in_=w1_raw[n][:].bitcast(I32).rearrange("p r (m t) -> p r t m", t=PACK),
+            )
+            return codes
+
+        def group_x(n):
             raw = x_raw[n][:].rearrange("p b (t q r) -> p r b q t", t=PACK, q=SPOTS, r=2)
-            grouped = work.tile([P, 3, POS, PACK], BF16, name="x_grouped", align_bytes=64)
-            by_batch = grouped[:].rearrange("p v (b q) t -> p v b q t", b=BATCH)
-            nc.scalar.copy(out=by_batch[:, RE], in_=raw[:, 0])
-            if n == 0:
-                nc.vector.tensor_copy(out=by_batch[:, IM], in_=raw[:, 1])
+            runs = []
+            for u, (q0, qn) in enumerate(RUNS):
+                grouped = work.tile(
+                    [P, 3, BATCH * qn, PACK], BF16, name="x_grouped%d" % u, align_bytes=64
+                )
+                by_batch = grouped[:].rearrange("p v (b q) t -> p v b q t", b=BATCH)
+                if n == 0:
+                    nc.scalar.copy(out=by_batch[:, RE], in_=raw[:, 0, :, q0 : q0 + qn, :])
+                    nc.vector.tensor_copy(out=by_batch[:, IM], in_=raw[:, 1, :, q0 : q0 + qn, :])
+                else:
+                    step = 128 // qn
+                    for variant, r in ((RE, 0), (IM, 1)):
+                        for b in range(0, BATCH, step):
+                            nc.gpsimd.tensor_scalar(
+                                out=by_batch[:, variant, b : b + step],
+                                in0=raw[:, r, b : b + step, q0 : q0 + qn, :],
+                                scalar1=1.0,
+                                scalar2=0.0,
+                                op0=MULT,
+                                op1=ADD,
+                            )
                 nc.vector.tensor_scalar_mul(
                     out=grouped[:, NEG_IM], in0=grouped[:, IM], scalar1=-1.0
                 )
-            else:
-                for b in range(BATCH):
-                    for variant, sign in ((IM, 1.0), (NEG_IM, -1.0)):
-                        nc.gpsimd.tensor_scalar(
-                            out=by_batch[:, variant, b],
-                            in0=raw[:, 1, b],
-                            scalar1=sign,
-                            scalar2=0.0,
-                            op0=MULT,
-                            op1=ADD,
-                        )
-            nc.scalar.copy(out=b1_all[:, n], in_=spread[:])
-            return grouped
-
-        def quantise_x(grouped):
-            codes = work.tile([P, 3 * POS], U32, name="x_codes", align_bytes=64)
-            scales = work.tile([P, 3 * POS], U8, name="x_scales", align_bytes=64)
-            quantise(grouped, POS, codes, scales, 0)
-            return codes, scales
-
-        def layer_1(n, x_codes, x_scales):
-            pre = []
-            for a in range(POS_TILES):
-                for part in range(2):
-                    acc = psum_mx.tile([P, BS], F32, name="acc_1", tag="acc")
-                    for i, (variant, w_part) in enumerate(PRODUCTS[part]):
-                        cols = slice(variant * POS + a * P, variant * POS + (a + 1) * P)
-                        nc.tensor.matmul_mx(
-                            out=acc[:],
-                            lhsT=x_codes[:, cols].bitcast(FP8X4),
-                            lhsT_scale=x_scales[:, cols],
-                            rhs=w1_codes[n][:, w_part, :].bitcast(FP8X4),
-                            rhs_scale=w1_planes[:, w_part * BLOCKS + n, :],
-                            start=(i == 0),
-                            stop=(i == 1),
-                        )
-                    biased = sums.tile([P, PACK, P], BF16, name="biased")
-                    nc.vector.tensor_tensor(
-                        out=biased[:],
-                        in0=acc[:].rearrange("p (j t) -> p t j", t=PACK),
-                        in1=b1_all[:, n, part, :].rearrange("p (j t) -> p t j", t=PACK),
-                        op=ADD,
-                    )
-                    pre.append(biased)
-            return pre
-
-        def transpose(pre):
-            runs = []
-            for first, width in RUNS:
-                grouped = work.tile(
-                    [P, 3, width, PACK], BF16, name="h_grouped%d" % width, align_bytes=64
-                )
-                for a in range(first // P, (first + width) // P):
-                    turned = psum_t.tile([P, 2, PACK, P], BF16, name="turned")
-                    for part in range(2):
-                        for t in range(PACK):
-                            nc.tensor.transpose(
-                                out=turned[:, part, t, :],
-                                in_=pre[2 * a + part][:, t, :],
-                                identity=identity[:],
-                            )
-                    nc.scalar.activation(
-                        out=grouped[:, RE : IM + 1, a * P - first : (a + 1) * P - first, :],
-                        in_=turned[:].rearrange("p r t c -> p r c t"),
-                        func=RELU,
-                    )
                 runs.append(grouped)
-            for grouped in runs:
-                nc.scalar.mul(out=grouped[:, NEG_IM], in_=grouped[:, IM], mul=-1.0)
             return runs
 
-        def quantise_h(runs):
-            codes = work.tile([P, 3 * POS], U32, name="h_codes", align_bytes=64)
-            scales = work.tile([P, 3 * POS], U8, name="h_scales", align_bytes=64)
-            for (first, width), grouped in zip(RUNS, runs):
-                quantise(grouped, width, codes, scales, 3 * first)
-            return codes, scales
+        def mx_pair(acc, codes, planes, n, tile_index, moving, first, width):
+            cols_w = slice(tile_index * P, (tile_index + 1) * P)
+            for w_part, start in ((0, width), (1, 0)):
+                cols = slice(first + start, first + start + 2 * width)
+                nc.tensor.matmul_mx(
+                    out=acc[:].rearrange("p r c -> p (r c)"),
+                    lhsT=codes[:, w_part, cols_w].bitcast(FP8X4),
+                    lhsT_scale=planes[4 * n : P, w_part, cols_w],
+                    rhs=moving[0][:, cols].bitcast(FP8X4),
+                    rhs_scale=moving[1][:, cols],
+                    start=(w_part == 0),
+                    stop=(w_part == 1),
+                )
 
-        def layer_2(n, h_codes, h_scales):
-            for m in range(OUT_TILES):
-                result = results.tile([P, POS, 2], F32, name="result")
-                for first, width in RUNS:
-                    acc = psum_mx.tile([P, 2, width], F32, name="acc_2_%d" % width, tag="acc")
-                    for w_part, start in ((0, width), (1, 0)):
-                        cols = slice(3 * first + start, 3 * first + start + 2 * width)
-                        nc.tensor.matmul_mx(
-                            out=acc[:].rearrange("p r c -> p (r c)"),
-                            lhsT=w2_codes[n][:, w_part, m * P : (m + 1) * P].bitcast(FP8X4),
-                            lhsT_scale=w2_planes[:, w_part * BLOCKS + n, m * P : (m + 1) * P],
-                            rhs=h_codes[:, cols].bitcast(FP8X4),
-                            rhs_scale=h_scales[:, cols],
-                            start=(w_part == 0),
-                            stop=(w_part == 1),
+        def layer_1(n, x_mx):
+            planar = []
+            for u, (q0, qn) in enumerate(RUNS):
+                width = BATCH * qn
+                hidden = work.tile([P, 2, PACK, width], BF16, name="h_planar%d" % u)
+                for t in range(PACK):
+                    acc = psum.tile([P, 2, width], F32, name="acc_1_%d" % u, tag="acc")
+                    mx_pair(acc, w1_codes[n], w1_planes, n, t, x_mx, 3 * BATCH * q0, width)
+                    for part in range(2):
+                        nc.scalar.activation(
+                            out=hidden[:, part, t, :],
+                            in_=acc[:, part, :],
+                            func=RELU,
+                            bias=b1_cols[:, part * BLOCKS + n, t : t + 1],
                         )
+                planar.append(hidden)
+            return planar
+
+        def group_h(planar):
+            runs = []
+            for u, (q0, qn) in enumerate(RUNS):
+                grouped = work.tile(
+                    [P, 3, BATCH * qn, PACK], BF16, name="h_grouped%d" % u, align_bytes=64
+                )
+                nc.scalar.copy(
+                    out=grouped[:, RE : IM + 1],
+                    in_=planar[u][:].rearrange("p r t c -> p r c t"),
+                )
+                nc.vector.tensor_scalar_mul(
+                    out=grouped[:, NEG_IM], in0=grouped[:, IM], scalar1=-1.0
+                )
+                runs.append(grouped)
+            return runs
+
+        def layer_2(n, h_mx):
+            for m in range(OUT_TILES):
+                result = results.tile([P, BATCH, SPOTS, 2], F32, name="result")
+                for u, (q0, qn) in enumerate(RUNS):
+                    width = BATCH * qn
+                    acc = psum.tile([P, 2, width], F32, name="acc_2_%d" % u, tag="acc")
+                    mx_pair(acc, w2_codes[n], w2_planes, n, m, h_mx, 3 * BATCH * q0, width)
                     nc.vector.tensor_tensor(
-                        out=result[:, first : first + width, :],
-                        in0=acc[:].rearrange("p r c -> p c r"),
+                        out=result[:, :, q0 : q0 + qn, :],
+                        in0=acc[:].rearrange("p r (b q) -> p b q r", b=BATCH),
                         in1=b2_cols[:, n * OUT_TILES + m, :]
                         .unsqueeze(1)
-                        .to_broadcast([P, width, 2]),
+                        .unsqueeze(1)
+                        .to_broadcast([P, BATCH, qn, 2]),
                         op=ADD,
                     )
                 channel = n * BS + m * P
                 nc.sync.dma_start(
                     out=out_rows[:, channel : channel + P, :].rearrange("b c f -> c b f"),
-                    in_=result[:].rearrange("p (b q) r -> p b (q r)", b=BATCH),
+                    in_=result[:].rearrange("p b q r -> p b (q r)"),
                 )
 
-        b1_rows = keep.tile([P, BS], BF16, name="b1_rows")
-        nc.vector.memset(b1_rows[:], 0.0)
         b2_rows = keep.tile([P, P], BF16, name="b2_rows")
         nc.vector.memset(b2_rows[:], 0.0)
+        b1_cols = keep.tile([P, 2 * BLOCKS, PACK], BF16, name="b1_cols")
         x_raw = [load_x(0)]
-        nc.scalar.dma_start(out=b1_rows[0 : 2 * BLOCKS, :], in_=b1.rearrange("r n k -> (r n) k"))
-        w1_planes = load_planes(w1_scales, "w1_planes")
-        w1_codes = [load_words(w1_words, 0, "w1_codes")]
+        nc.scalar.dma_start(out=b1_cols[:], in_=b1.rearrange("r n (p t) -> p (r n) t", t=PACK))
+        w1_planes_raw = load_planes(w1_scales, "w1_planes_raw")
+        w1_raw = [load_words(w1_words, 0, "w1_raw")]
         x_raw.append(load_x(1))
         nc.scalar.dma_start(
             out=b2_rows[0 : 2 * BLOCKS * OUT_TILES, :],
@@ -235,7 +219,7 @@ def tile_scatteringmodule_pa_e_kernel(
         w2_planes = load_planes(w2_scales, "w2_planes")
         w2_codes = [load_words(w2_words, 0, "w2_codes")]
         for n in range(1, BLOCKS):
-            w1_codes.append(load_words(w1_words, n, "w1_codes"))
+            w1_raw.append(load_words(w1_words, n, "w1_raw"))
             if n + 1 < BLOCKS:
                 x_raw.append(load_x(n + 1))
             w2_codes.append(load_words(w2_words, n, "w2_codes"))
@@ -243,9 +227,14 @@ def tile_scatteringmodule_pa_e_kernel(
         identity = keep.tile([P, P], BF16, name="identity")
         make_identity(nc, identity[:])
 
-        b1_all = keep.tile([P, BLOCKS, 2, BS], BF16, name="b1_all")
+        w1_planes = keep.tile([P, 2, BS], U8, name="w1_planes", align_bytes=64)
+        for t in range(PACK):
+            nc.vector.tensor_copy(
+                out=w1_planes[:, :, t * P : (t + 1) * P],
+                in_=w1_planes_raw[:].rearrange("p r (m t) -> p r m t", t=PACK)[:, :, :, t],
+            )
 
-        b2_turned = psum_t.tile([P, P], BF16, name="b2_turned", tag="turned")
+        b2_turned = psum.tile([P, P], BF16, name="b2_turned", tag="acc")
         nc.tensor.transpose(out=b2_turned[:], in_=b2_rows[:], identity=identity[:])
         b2_cols = keep.tile([P, BLOCKS * OUT_TILES, 2], F32, name="b2_cols")
         nc.vector.tensor_copy(
@@ -253,19 +242,20 @@ def tile_scatteringmodule_pa_e_kernel(
             in_=b2_turned[:, 0 : 2 * BLOCKS * OUT_TILES].rearrange("p (r g) -> p g r", r=2),
         )
 
-        x_grouped = [prepare(0), prepare(1)]
-        x_mx = quantise_x(x_grouped[0])
-        pre = layer_1(0, x_mx[0], x_mx[1])
-        h_mx = None
+        x_grouped = group_x(0)
+        w1_codes = [permute_w1(0)]
+        x_mx = quantise_runs(x_grouped, "x")
+        planar = layer_1(0, x_mx)
+        x_grouped = group_x(1)
+        w1_codes.append(permute_w1(1))
         for n in range(BLOCKS):
-            runs = transpose(pre)
+            h_grouped = group_h(planar)
+            if n + 1 < BLOCKS:
+                x_mx = quantise_runs(x_grouped, "x")
+            h_mx = quantise_runs(h_grouped, "h")
+            if n + 1 < BLOCKS:
+                planar = layer_1(n + 1, x_mx)
             if n + 2 < BLOCKS:
-                x_grouped.append(prepare(n + 2))
-            if n + 1 < BLOCKS:
-                x_mx = quantise_x(x_grouped[n + 1])
-            if n > 0:
-                layer_2(n - 1, h_mx[0], h_mx[1])
-            h_mx = quantise_h(runs)
-            if n + 1 < BLOCKS:
-                pre = layer_1(n + 1, x_mx[0], x_mx[1])
-        layer_2(BLOCKS - 1, h_mx[0], h_mx[1])
+                x_grouped = group_x(n + 2)
+                w1_codes.append(permute_w1(n + 2))
+            layer_2(n, h_mx)

@@ -22,8 +22,10 @@ BLOCKS = 4
 BS = 512
 OUT_TILES = BS // P
 NEG_IM, RE, IM = 0, 1, 2
-RUNS = ((0, 64), (64, 32))
+RUNS = ((0, 256), (256, 128))
 MAX_QUANTIZE_WORDS = 1024
+X_ENGINES = ("SV", "SG", "GV", "GG")
+H_ENGINES = ("SV", "SG", "SG", "SG")
 
 FLOPS = 2 * 8 * BLOCKS * POS * BS * BS
 
@@ -79,9 +81,24 @@ def tile_scatteringmodule_pa_e_kernel(
                     )
             return planes
 
-        def quantise(grouped, width, codes, scales, first):
-            flat = grouped[:].rearrange("p v c t -> p (v c t)")
-            for start, columns in ((width, 2 * width), (0, width)):
+        def lay_side_by_side(engine, target, source):
+            if engine == "S":
+                nc.scalar.copy(out=target, in_=source)
+            elif engine == "V":
+                nc.vector.tensor_copy(out=target, in_=source)
+            else:
+                for g in range(target.shape[1]):
+                    nc.gpsimd.tensor_scalar(
+                        out=target[:, g],
+                        in0=source[:, g],
+                        scalar1=1.0,
+                        scalar2=0.0,
+                        op0=MULT,
+                        op1=ADD,
+                    )
+
+        def quantise(flat, codes, scales, first, spans):
+            for start, columns in spans:
                 for cut in powers_of_two(columns):
                     nc.vector.quantize_mx(
                         out=codes[:, first + start : first + start + cut].bitcast(FP8X4),
@@ -90,56 +107,34 @@ def tile_scatteringmodule_pa_e_kernel(
                     )
                     start += cut
 
-        def quantise_runs(runs, name):
-            codes = work.tile([P, 3 * POS], U32, name=name + "_codes", align_bytes=64)
-            scales = work.tile([P, 3 * POS], U8, name=name + "_scales", align_bytes=64)
-            for (q0, qn), grouped in zip(RUNS, runs):
-                quantise(grouped, BATCH * qn, codes, scales, 3 * BATCH * q0)
-            return codes, scales
-
-        def permute_w1(n):
-            codes = keep.tile([P, 2, BS], U32, name="w1_codes%d" % n, align_bytes=64)
-            nc.vector.tensor_copy(
-                out=codes[:].bitcast(I32).rearrange("p r (t m) -> p r t m", t=PACK),
-                in_=w1_raw[n][:].bitcast(I32).rearrange("p r (m t) -> p r t m", t=PACK),
-            )
-            return codes
-
         def group_x(n):
             raw = x_raw[n][:].rearrange("p b (t q r) -> p r b q t", t=PACK, q=SPOTS, r=2)
-            runs = []
-            for u, (q0, qn) in enumerate(RUNS):
-                grouped = work.tile(
-                    [P, 3, BATCH * qn, PACK], BF16, name="x_grouped%d" % u, align_bytes=64
-                )
-                by_batch = grouped[:].rearrange("p v (b q) t -> p v b q t", b=BATCH)
-                if n == 0:
-                    nc.scalar.copy(out=by_batch[:, RE], in_=raw[:, 0, :, q0 : q0 + qn, :])
-                    nc.vector.tensor_copy(out=by_batch[:, IM], in_=raw[:, 1, :, q0 : q0 + qn, :])
-                else:
-                    step = 128 // qn
-                    for variant, r in ((RE, 0), (IM, 1)):
-                        for b in range(0, BATCH, step):
-                            nc.gpsimd.tensor_scalar(
-                                out=by_batch[:, variant, b : b + step],
-                                in0=raw[:, r, b : b + step, q0 : q0 + qn, :],
-                                scalar1=1.0,
-                                scalar2=0.0,
-                                op0=MULT,
-                                op1=ADD,
-                            )
-                nc.vector.tensor_scalar_mul(
-                    out=grouped[:, NEG_IM], in0=grouped[:, IM], scalar1=-1.0
-                )
-                runs.append(grouped)
-            return runs
+            grouped = keep.tile([P, 3, POS, PACK], BF16, name="x_grouped%d" % n, align_bytes=64)
+            by_batch = grouped[:].rearrange("p v (b q) t -> p v b q t", b=BATCH)
+            lay_side_by_side(X_ENGINES[n][0], by_batch[:, RE], raw[:, 0])
+            lay_side_by_side(X_ENGINES[n][1], by_batch[:, IM], raw[:, 1])
+            return grouped
 
-        def mx_pair(acc, codes, planes, n, tile_index, moving, first, width):
+        def prepare_x(n, grouped):
+            nc.vector.tensor_scalar_mul(out=grouped[:, NEG_IM], in0=grouped[:, IM], scalar1=-1.0)
+            permuted = keep.tile([P, 2, BS], U32, name="w1_codes%d" % n, align_bytes=64)
+            nc.vector.tensor_copy(
+                out=permuted[:].bitcast(I32).rearrange("p r (t m) -> p r t m", t=PACK),
+                in_=w1_raw[n][:].bitcast(I32).rearrange("p r (m t) -> p r t m", t=PACK),
+            )
+            codes = keep.tile([P, 3 * POS], U32, name="x_codes%d" % n, align_bytes=64)
+            scales = keep.tile([P, 3 * POS], U8, name="x_scales%d" % n, align_bytes=64)
+            quantise(
+                grouped[:].rearrange("p v c t -> p (v c t)"), codes, scales, 0, ((0, 3 * POS),)
+            )
+            return permuted, (codes, scales)
+
+        def mx_pair(acc, codes, planes, n, tile_index, moving, re_im, neg_re, columns):
             cols_w = slice(tile_index * P, (tile_index + 1) * P)
-            for w_part, start in ((0, width), (1, 0)):
-                cols = slice(first + start, first + start + 2 * width)
+            for w_part, start in ((0, re_im), (1, neg_re)):
+                cols = slice(start, start + columns)
                 nc.tensor.matmul_mx(
-                    out=acc[:].rearrange("p r c -> p (r c)"),
+                    out=acc,
                     lhsT=codes[:, w_part, cols_w].bitcast(FP8X4),
                     lhsT_scale=planes[4 * n : P, w_part, cols_w],
                     rhs=moving[0][:, cols].bitcast(FP8X4),
@@ -148,84 +143,118 @@ def tile_scatteringmodule_pa_e_kernel(
                     stop=(w_part == 1),
                 )
 
-        def layer_1(n, x_mx):
-            planar = []
-            for u, (q0, qn) in enumerate(RUNS):
-                width = BATCH * qn
-                hidden = work.tile([P, 2, PACK, width], BF16, name="h_planar%d" % u)
-                for t in range(PACK):
-                    acc = psum.tile([P, 2, width], F32, name="acc_1_%d" % u, tag="acc")
-                    mx_pair(acc, w1_codes[n], w1_planes, n, t, x_mx, 3 * BATCH * q0, width)
-                    for part in range(2):
-                        nc.scalar.activation(
-                            out=hidden[:, part, t, :],
-                            in_=acc[:, part, :],
-                            func=RELU,
-                            bias=b1_cols[:, part * BLOCKS + n, t : t + 1],
-                        )
-                planar.append(hidden)
-            return planar
+        def layer_1(n):
+            hidden = work.tile([P, 2, PACK, POS], BF16, name="h_planar")
+            for t in range(PACK):
+                wide = psum.tile([P, 512], F32, name="acc_1_wide", tag="acc")
+                mx_pair(wide[:], w1_codes[n], w1_planes, n, t, x_mx[n], POS, 0, 512)
+                narrow = psum.tile([P, 256], F32, name="acc_1_narrow", tag="acc")
+                mx_pair(narrow[:], w1_codes[n], w1_planes, n, t, x_mx[n], POS + 512, 512, 256)
+                for part, target, source in (
+                    (0, hidden[:, 0, t, :], wide[:, 0:POS]),
+                    (1, hidden[:, 1, t, 0 : 512 - POS], wide[:, POS:512]),
+                    (1, hidden[:, 1, t, 512 - POS : POS], narrow[:]),
+                ):
+                    nc.scalar.activation(
+                        out=target,
+                        in_=source,
+                        func=RELU,
+                        bias=b1_cols[:, part * BLOCKS + n, t : t + 1],
+                    )
+            return hidden
 
-        def group_h(planar):
-            runs = []
-            for u, (q0, qn) in enumerate(RUNS):
+        def prepare_h(n, hidden):
+            codes = work.tile([P, 3 * POS], U32, name="h_codes", align_bytes=64)
+            scales = work.tile([P, 3 * POS], U8, name="h_scales", align_bytes=64)
+            for u, (first, width) in enumerate(RUNS):
                 grouped = work.tile(
-                    [P, 3, BATCH * qn, PACK], BF16, name="h_grouped%d" % u, align_bytes=64
+                    [P, 3, width, PACK], BF16, name="h_grouped%d" % u, align_bytes=64
                 )
-                nc.scalar.copy(
-                    out=grouped[:, RE : IM + 1],
-                    in_=planar[u][:].rearrange("p r t c -> p r c t"),
-                )
+                for part, variant in ((0, RE), (1, IM)):
+                    lay_side_by_side(
+                        H_ENGINES[n][part],
+                        grouped[:, variant].rearrange("p (g c) t -> p g c t", c=P),
+                        hidden[:, part, :, first : first + width].rearrange(
+                            "p t (g c) -> p g c t", c=P
+                        ),
+                    )
                 nc.vector.tensor_scalar_mul(
                     out=grouped[:, NEG_IM], in0=grouped[:, IM], scalar1=-1.0
                 )
-                runs.append(grouped)
-            return runs
+                quantise(
+                    grouped[:].rearrange("p v c t -> p (v c t)"),
+                    codes,
+                    scales,
+                    3 * first,
+                    ((width, 2 * width), (0, width)),
+                )
+            return codes, scales
 
         def layer_2(n, h_mx):
             for m in range(OUT_TILES):
-                result = results.tile([P, BATCH, SPOTS, 2], F32, name="result")
-                for u, (q0, qn) in enumerate(RUNS):
-                    width = BATCH * qn
+                result = results.tile([P, POS, 2], F32, name="result")
+                for u, (first, width) in enumerate(RUNS):
                     acc = psum.tile([P, 2, width], F32, name="acc_2_%d" % u, tag="acc")
-                    mx_pair(acc, w2_codes[n], w2_planes, n, m, h_mx, 3 * BATCH * q0, width)
+                    mx_pair(
+                        acc[:].rearrange("p r c -> p (r c)"),
+                        w2_codes[n],
+                        w2_planes,
+                        n,
+                        m,
+                        h_mx,
+                        3 * first + width,
+                        3 * first,
+                        2 * width,
+                    )
                     nc.vector.tensor_tensor(
-                        out=result[:, :, q0 : q0 + qn, :],
-                        in0=acc[:].rearrange("p r (b q) -> p b q r", b=BATCH),
+                        out=result[:, first : first + width, :],
+                        in0=acc[:].rearrange("p r c -> p c r"),
                         in1=b2_cols[:, n * OUT_TILES + m, :]
                         .unsqueeze(1)
-                        .unsqueeze(1)
-                        .to_broadcast([P, BATCH, qn, 2]),
+                        .to_broadcast([P, width, 2]),
                         op=ADD,
                     )
                 channel = n * BS + m * P
                 nc.sync.dma_start(
                     out=out_rows[:, channel : channel + P, :].rearrange("b c f -> c b f"),
-                    in_=result[:].rearrange("p b q r -> p b (q r)"),
+                    in_=result[:].rearrange("p (b q) r -> p b (q r)", b=BATCH),
                 )
 
         b2_rows = keep.tile([P, P], BF16, name="b2_rows")
         nc.vector.memset(b2_rows[:], 0.0)
         b1_cols = keep.tile([P, 2 * BLOCKS, PACK], BF16, name="b1_cols")
         x_raw = [load_x(0)]
-        nc.scalar.dma_start(out=b1_cols[:], in_=b1.rearrange("r n (p t) -> p (r n) t", t=PACK))
-        w1_planes_raw = load_planes(w1_scales, "w1_planes_raw")
         w1_raw = [load_words(w1_words, 0, "w1_raw")]
         x_raw.append(load_x(1))
+        w1_planes_raw = load_planes(w1_scales, "w1_planes_raw")
+        nc.scalar.dma_start(out=b1_cols[:], in_=b1.rearrange("r n (p t) -> p (r n) t", t=PACK))
+        x_raw.append(load_x(2))
+        w1_raw.append(load_words(w1_words, 1, "w1_raw"))
+        x_raw.append(load_x(3))
+        w1_raw.append(load_words(w1_words, 2, "w1_raw"))
         nc.scalar.dma_start(
             out=b2_rows[0 : 2 * BLOCKS * OUT_TILES, :],
             in_=b2.rearrange("r n (m j) -> (r n m) j", j=P),
         )
         w2_planes = load_planes(w2_scales, "w2_planes")
         w2_codes = [load_words(w2_words, 0, "w2_codes")]
+        w1_raw.append(load_words(w1_words, 3, "w1_raw"))
         for n in range(1, BLOCKS):
-            w1_raw.append(load_words(w1_words, n, "w1_raw"))
-            if n + 1 < BLOCKS:
-                x_raw.append(load_x(n + 1))
             w2_codes.append(load_words(w2_words, n, "w2_codes"))
 
         identity = keep.tile([P, P], BF16, name="identity")
         make_identity(nc, identity[:])
+
+        w1_codes = []
+        x_mx = []
+
+        def x_step(n):
+            permuted, mx = prepare_x(n, x_grouped[n])
+            w1_codes.append(permuted)
+            x_mx.append(mx)
+
+        x_grouped = [group_x(0)]
+        x_step(0)
 
         w1_planes = keep.tile([P, 2, BS], U8, name="w1_planes", align_bytes=64)
         for t in range(PACK):
@@ -233,6 +262,12 @@ def tile_scatteringmodule_pa_e_kernel(
                 out=w1_planes[:, :, t * P : (t + 1) * P],
                 in_=w1_planes_raw[:].rearrange("p r (m t) -> p r m t", t=PACK)[:, :, :, t],
             )
+
+        for n in range(1, BLOCKS):
+            x_grouped.append(group_x(n))
+        hidden = {0: layer_1(0)}
+        x_step(1)
+        x_step(2)
 
         b2_turned = psum.tile([P, P], BF16, name="b2_turned", tag="acc")
         nc.tensor.transpose(out=b2_turned[:], in_=b2_rows[:], identity=identity[:])
@@ -242,20 +277,12 @@ def tile_scatteringmodule_pa_e_kernel(
             in_=b2_turned[:, 0 : 2 * BLOCKS * OUT_TILES].rearrange("p (r g) -> p g r", r=2),
         )
 
-        x_grouped = group_x(0)
-        w1_codes = [permute_w1(0)]
-        x_mx = quantise_runs(x_grouped, "x")
-        planar = layer_1(0, x_mx)
-        x_grouped = group_x(1)
-        w1_codes.append(permute_w1(1))
+        h_mx = {0: prepare_h(0, hidden[0])}
+        hidden[1] = layer_1(1)
+        x_step(3)
         for n in range(BLOCKS):
-            h_grouped = group_h(planar)
+            layer_2(n, h_mx[n])
             if n + 1 < BLOCKS:
-                x_mx = quantise_runs(x_grouped, "x")
-            h_mx = quantise_runs(h_grouped, "h")
-            if n + 1 < BLOCKS:
-                planar = layer_1(n + 1, x_mx)
+                h_mx[n + 1] = prepare_h(n + 1, hidden[n + 1])
             if n + 2 < BLOCKS:
-                x_grouped = group_x(n + 2)
-                w1_codes.append(permute_w1(n + 2))
-            layer_2(n, h_mx)
+                hidden[n + 2] = layer_1(n + 2)

@@ -24,8 +24,8 @@ OUT_TILES = BS // P
 NEG_IM, RE, IM = 0, 1, 2
 RUNS = ((0, 256), (256, 128))
 MAX_QUANTIZE_WORDS = 1024
-X_ENGINES = ("SV", "SG", "GV", "GG")
-H_ENGINES = ("SV", "SG", "SG", "SG")
+X_ENGINES = ("SV", "SV", "SV", "SV")
+H_ENGINES = ("SV", "SS", "SS", "SS")
 
 FLOPS = 2 * 8 * BLOCKS * POS * BS * BS
 

@@ -173,9 +173,9 @@ def tile_scatteringmodule_pa_e_kernel(
                 for part, variant in ((0, RE), (1, IM)):
                     lay_side_by_side(
                         H_ENGINES[n][part],
-                        grouped[:, variant].rearrange("p (g c) t -> p g c t", c=P),
+                        grouped[:, variant].rearrange("p (c i) t -> p c t i", i=4),
                         hidden[:, part, :, first : first + width].rearrange(
-                            "p t (g c) -> p g c t", c=P
+                            "p t (c i) -> p c t i", i=4
                         ),
                     )
                 nc.vector.tensor_scalar_mul(

@@ -108,9 +108,11 @@ def tile_scatteringmodule_pa_e_kernel(
                     start += cut
 
         def group_x(n):
-            raw = x_raw[n][:].rearrange("p b (t q r) -> p r b q t", t=PACK, q=SPOTS, r=2)
+            raw = x_raw[n][:].rearrange(
+                "p b (t c i r) -> p r b c t i", t=PACK, c=SPOTS // 4, i=4, r=2
+            )
             grouped = keep.tile([P, 3, POS, PACK], BF16, name="x_grouped%d" % n, align_bytes=64)
-            by_batch = grouped[:].rearrange("p v (b q) t -> p v b q t", b=BATCH)
+            by_batch = grouped[:].rearrange("p v (b c i) t -> p v b c t i", b=BATCH, i=4)
             lay_side_by_side(X_ENGINES[n][0], by_batch[:, RE], raw[:, 0])
             lay_side_by_side(X_ENGINES[n][1], by_batch[:, IM], raw[:, 1])
             return grouped

@@ -121,8 +121,8 @@ def tile_scatteringmodule_pa_e_kernel(
             nc.vector.tensor_scalar_mul(out=grouped[:, NEG_IM], in0=grouped[:, IM], scalar1=-1.0)
             permuted = keep.tile([P, 2, BS], U32, name="w1_codes%d" % n, align_bytes=64)
             nc.vector.tensor_copy(
-                out=permuted[:].bitcast(I32).rearrange("p r (t m) -> p r t m", t=PACK),
-                in_=w1_raw[n][:].bitcast(I32).rearrange("p r (m t) -> p r t m", t=PACK),
+                out=permuted[:].bitcast(I32).rearrange("p r (t m i) -> p r m t i", t=PACK, i=4),
+                in_=w1_raw[n][:].bitcast(I32).rearrange("p r (m i t) -> p r m t i", t=PACK, i=4),
             )
             codes = keep.tile([P, 3 * POS], U32, name="x_codes%d" % n, align_bytes=64)
             scales = keep.tile([P, 3 * POS], U8, name="x_scales%d" % n, align_bytes=64)

@@ -247,6 +247,7 @@ def tile_scatteringmodule_pa_e_kernel(
         identity = keep.tile([P, P], BF16, name="identity")
         make_identity(nc, identity[:])
 
+        ctx.enter_context(tc.manual_schedule())
         w1_codes = []
         x_mx = []
 

@@ -175,9 +175,9 @@ def tile_scatteringmodule_pa_e_kernel(
                 for part, variant in ((0, RE), (1, IM)):
                     lay_side_by_side(
                         H_ENGINES[n][part],
-                        grouped[:, variant].rearrange("p (c i) t -> p c t i", i=4),
+                        grouped[:, variant].rearrange("p (c i) t -> p c t i", i=8),
                         hidden[:, part, :, first : first + width].rearrange(
-                            "p t (c i) -> p c t i", i=4
+                            "p t (c i) -> p c t i", i=8
                         ),
                     )
                 nc.vector.tensor_scalar_mul(

@@ -25,7 +25,8 @@ NEG_IM, RE, IM = 0, 1, 2
 RUNS = ((0, 256), (256, 128))
 MAX_QUANTIZE_WORDS = 1024
 X_ENGINES = ("SV", "SV", "SV", "SV")
-H_ENGINES = ("SV", "SS", "SS", "SS")
+H_ENGINES = ("SV", "SG", "SG", "SG")
+G_POSITIONS = 128
 
 FLOPS = 2 * 8 * BLOCKS * POS * BS * BS
 
@@ -87,10 +88,10 @@ def tile_scatteringmodule_pa_e_kernel(
             elif engine == "V":
                 nc.vector.tensor_copy(out=target, in_=source)
             else:
-                for g in range(target.shape[1]):
+                for g in range(0, target.shape[1], G_POSITIONS):
                     nc.gpsimd.tensor_scalar(
-                        out=target[:, g],
-                        in0=source[:, g],
+                        out=target[:, g : g + G_POSITIONS],
+                        in0=source[:, g : g + G_POSITIONS],
                         scalar1=1.0,
                         scalar2=0.0,
                         op0=MULT,
@@ -173,13 +174,20 @@ def tile_scatteringmodule_pa_e_kernel(
                     [P, 3, width, PACK], BF16, name="h_grouped%d" % u, align_bytes=64
                 )
                 for part, variant in ((0, RE), (1, IM)):
-                    lay_side_by_side(
-                        H_ENGINES[n][part],
-                        grouped[:, variant].rearrange("p (c i) t -> p c t i", i=8),
-                        hidden[:, part, :, first : first + width].rearrange(
-                            "p t (c i) -> p c t i", i=8
-                        ),
-                    )
+                    if H_ENGINES[n][part] == "G":
+                        lay_side_by_side(
+                            "G",
+                            grouped[:, variant],
+                            hidden[:, part, :, first : first + width].rearrange("p t c -> p c t"),
+                        )
+                    else:
+                        lay_side_by_side(
+                            H_ENGINES[n][part],
+                            grouped[:, variant].rearrange("p (c i) t -> p c t i", i=8),
+                            hidden[:, part, :, first : first + width].rearrange(
+                                "p t (c i) -> p c t i", i=8
+                            ),
+                        )
                 nc.vector.tensor_scalar_mul(
                     out=grouped[:, NEG_IM], in0=grouped[:, IM], scalar1=-1.0
                 )

@@ -24,7 +24,7 @@ OUT_TILES = BS // P
 NEG_IM, RE, IM = 0, 1, 2
 RUNS = ((0, 256), (256, 128))
 MAX_QUANTIZE_WORDS = 1024
-X_ENGINES = ("SV", "SV", "SV", "SV")
+X_ENGINES = ("SV", "SV", "SV", "SS")
 H_ENGINES = ("SV", "SG", "SG", "SG")
 G_POSITIONS = 128
 
@@ -166,39 +166,41 @@ def tile_scatteringmodule_pa_e_kernel(
                     )
             return hidden
 
-        def prepare_h(n, hidden):
+        def lay_h(n, hidden, u):
+            first, width = RUNS[u]
+            grouped = work.tile([P, 3, width, PACK], BF16, name="h_grouped%d" % u, align_bytes=64)
+            for part, variant in ((0, RE), (1, IM)):
+                if H_ENGINES[n][part] == "G":
+                    lay_side_by_side(
+                        "G",
+                        grouped[:, variant],
+                        hidden[:, part, :, first : first + width].rearrange("p t c -> p c t"),
+                    )
+                else:
+                    lay_side_by_side(
+                        H_ENGINES[n][part],
+                        grouped[:, variant].rearrange("p (c i) t -> p c t i", i=8),
+                        hidden[:, part, :, first : first + width].rearrange(
+                            "p t (c i) -> p c t i", i=8
+                        ),
+                    )
+            return grouped
+
+        def new_h_mx():
             codes = work.tile([P, 3 * POS], U32, name="h_codes", align_bytes=64)
             scales = work.tile([P, 3 * POS], U8, name="h_scales", align_bytes=64)
-            for u, (first, width) in enumerate(RUNS):
-                grouped = work.tile(
-                    [P, 3, width, PACK], BF16, name="h_grouped%d" % u, align_bytes=64
-                )
-                for part, variant in ((0, RE), (1, IM)):
-                    if H_ENGINES[n][part] == "G":
-                        lay_side_by_side(
-                            "G",
-                            grouped[:, variant],
-                            hidden[:, part, :, first : first + width].rearrange("p t c -> p c t"),
-                        )
-                    else:
-                        lay_side_by_side(
-                            H_ENGINES[n][part],
-                            grouped[:, variant].rearrange("p (c i) t -> p c t i", i=8),
-                            hidden[:, part, :, first : first + width].rearrange(
-                                "p t (c i) -> p c t i", i=8
-                            ),
-                        )
-                nc.vector.tensor_scalar_mul(
-                    out=grouped[:, NEG_IM], in0=grouped[:, IM], scalar1=-1.0
-                )
-                quantise(
-                    grouped[:].rearrange("p v c t -> p (v c t)"),
-                    codes,
-                    scales,
-                    3 * first,
-                    ((width, 2 * width), (0, width)),
-                )
             return codes, scales
+
+        def quantise_h(grouped, u, mx):
+            first, width = RUNS[u]
+            nc.vector.tensor_scalar_mul(out=grouped[:, NEG_IM], in0=grouped[:, IM], scalar1=-1.0)
+            quantise(
+                grouped[:].rearrange("p v c t -> p (v c t)"),
+                mx[0],
+                mx[1],
+                3 * first,
+                ((width, 2 * width), (0, width)),
+            )
 
         def layer_2(n, h_mx):
             for m in range(OUT_TILES):
@@ -266,6 +268,7 @@ def tile_scatteringmodule_pa_e_kernel(
 
         x_grouped = [group_x(0)]
         x_step(0)
+        x_grouped.append(group_x(1))
 
         w1_planes = keep.tile([P, 2, BS], U8, name="w1_planes", align_bytes=64)
         for t in range(PACK):
@@ -274,11 +277,9 @@ def tile_scatteringmodule_pa_e_kernel(
                 in_=w1_planes_raw[:].rearrange("p r (m t) -> p r m t", t=PACK)[:, :, :, t],
             )
 
-        for n in range(1, BLOCKS):
-            x_grouped.append(group_x(n))
         hidden = {0: layer_1(0)}
         x_step(1)
-        x_step(2)
+        x_grouped.append(group_x(2))
 
         b2_turned = psum.tile([P, P], BF16, name="b2_turned", tag="acc")
         nc.tensor.transpose(out=b2_turned[:], in_=b2_rows[:], identity=identity[:])
@@ -287,13 +288,25 @@ def tile_scatteringmodule_pa_e_kernel(
             out=b2_cols[:],
             in_=b2_turned[:, 0 : 2 * BLOCKS * OUT_TILES].rearrange("p (r g) -> p g r", r=2),
         )
+        x_step(2)
 
-        h_mx = {0: prepare_h(0, hidden[0])}
+        h_mx = {0: new_h_mx()}
+        for u in range(len(RUNS)):
+            quantise_h(lay_h(0, hidden[0], u), u, h_mx[0])
         hidden[1] = layer_1(1)
-        x_step(3)
         for n in range(BLOCKS):
+            if n + 1 < BLOCKS:
+                h_grouped = []
+                for u in range(len(RUNS)):
+                    h_grouped.append(lay_h(n + 1, hidden[n + 1], u))
+            if n == 0:
+                x_grouped.append(group_x(3))
             layer_2(n, h_mx[n])
             if n + 1 < BLOCKS:
-                h_mx[n + 1] = prepare_h(n + 1, hidden[n + 1])
+                h_mx[n + 1] = new_h_mx()
+                for u in range(len(RUNS)):
+                    quantise_h(h_grouped[u], u, h_mx[n + 1])
+            if n == 0:
+                x_step(3)
             if n + 2 < BLOCKS:
                 hidden[n + 2] = layer_1(n + 2)

@@ -69,18 +69,20 @@ def tile_scatteringmodule_pa_e_kernel(
             nc.sync.dma_start(out=codes[:].bitcast(I32), in_=by_part[:, :, n, :])
             return codes
 
-        def load_planes(scales, name):
+        def new_planes(name):
             planes = keep.tile([P, 2, BS], U8, name=name, align_bytes=64)
             nc.vector.memset(planes[:].bitcast(I32), 0)
-            for quad in range(4):
-                for part in range(2):
-                    nc.sync.dma_start(
-                        out=planes[32 * quad : 32 * quad + 16, part, :].bitcast(I32),
-                        in_=scales[
-                            part * BLOCKS : (part + 1) * BLOCKS, 4 * quad : 4 * quad + 4, :
-                        ].bitcast(I32),
-                    )
             return planes
+
+        def load_planes(scales, planes, pieces):
+            for piece in pieces:
+                quad, part = divmod(piece, 2)
+                nc.sync.dma_start(
+                    out=planes[32 * quad : 32 * quad + 16, part, :].bitcast(I32),
+                    in_=scales[
+                        part * BLOCKS : (part + 1) * BLOCKS, 4 * quad : 4 * quad + 4, :
+                    ].bitcast(I32),
+                )
 
         def lay_side_by_side(engine, target, source):
             if engine == "S":
@@ -108,29 +110,35 @@ def tile_scatteringmodule_pa_e_kernel(
                     )
                     start += cut
 
-        def group_x(n):
+        def new_x_grouped(n):
+            return keep.tile([P, 3, POS, PACK], BF16, name="x_grouped%d" % n, align_bytes=64)
+
+        def group_x(n, part):
             raw = x_raw[n][:].rearrange(
                 "p b (t c i r) -> p r b c t i", t=PACK, c=SPOTS // 4, i=4, r=2
             )
-            grouped = keep.tile([P, 3, POS, PACK], BF16, name="x_grouped%d" % n, align_bytes=64)
-            by_batch = grouped[:].rearrange("p v (b c i) t -> p v b c t i", b=BATCH, i=4)
-            lay_side_by_side(X_ENGINES[n][0], by_batch[:, RE], raw[:, 0])
-            lay_side_by_side(X_ENGINES[n][1], by_batch[:, IM], raw[:, 1])
-            return grouped
+            by_batch = x_grouped[n][:].rearrange("p v (b c i) t -> p v b c t i", b=BATCH, i=4)
+            lay_side_by_side(X_ENGINES[n][part], by_batch[:, (RE, IM)[part]], raw[:, part])
 
-        def prepare_x(n, grouped):
+        def negate_x(n):
+            grouped = x_grouped[n]
             nc.vector.tensor_scalar_mul(out=grouped[:, NEG_IM], in0=grouped[:, IM], scalar1=-1.0)
+
+        def permute_w1(n):
             permuted = keep.tile([P, 2, BS], U32, name="w1_codes%d" % n, align_bytes=64)
             nc.vector.tensor_copy(
                 out=permuted[:].bitcast(I32).rearrange("p r (t m i) -> p r m t i", t=PACK, i=4),
                 in_=w1_raw[n][:].bitcast(I32).rearrange("p r (m i t) -> p r m t i", t=PACK, i=4),
             )
+            w1_codes[n] = permuted
+
+        def quantise_x(n):
             codes = keep.tile([P, 3 * POS], U32, name="x_codes%d" % n, align_bytes=64)
             scales = keep.tile([P, 3 * POS], U8, name="x_scales%d" % n, align_bytes=64)
             quantise(
-                grouped[:].rearrange("p v c t -> p (v c t)"), codes, scales, 0, ((0, 3 * POS),)
+                x_grouped[n][:].rearrange("p v c t -> p (v c t)"), codes, scales, 0, ((0, 3 * POS),)
             )
-            return permuted, (codes, scales)
+            x_mx[n] = (codes, scales)
 
         def mx_pair(acc, codes, planes, n, tile_index, moving, re_im, neg_re, columns):
             cols_w = slice(tile_index * P, (tile_index + 1) * P)
@@ -232,43 +240,72 @@ def tile_scatteringmodule_pa_e_kernel(
                     in_=result[:].rearrange("p (b q) r -> p b (q r)", b=BATCH),
                 )
 
-        b2_rows = keep.tile([P, P], BF16, name="b2_rows")
-        nc.vector.memset(b2_rows[:], 0.0)
-        b1_cols = keep.tile([P, 2 * BLOCKS, PACK], BF16, name="b1_cols")
+        bias_rows = keep.tile([P, BS + P], BF16, name="bias_rows")
+        nc.vector.memset(bias_rows[:], 0.0)
+        nc.scalar.dma_start(out=bias_rows[0 : 2 * BLOCKS, 0:BS], in_=b1.rearrange("r n c -> (r n) c"))
+        nc.scalar.dma_start(
+            out=bias_rows[0 : 2 * BLOCKS * OUT_TILES, BS : BS + P],
+            in_=b2.rearrange("r n (m j) -> (r n m) j", j=P),
+        )
+        w1_planes_raw = new_planes("w1_planes_raw")
+        w2_planes = new_planes("w2_planes")
         x_raw = [load_x(0)]
         w1_raw = [load_words(w1_words, 0, "w1_raw")]
         x_raw.append(load_x(1))
-        w1_planes_raw = load_planes(w1_scales, "w1_planes_raw")
-        nc.scalar.dma_start(out=b1_cols[:], in_=b1.rearrange("r n (p t) -> p (r n) t", t=PACK))
-        x_raw.append(load_x(2))
+        load_planes(w1_scales, w1_planes_raw, range(0, 5))
         w1_raw.append(load_words(w1_words, 1, "w1_raw"))
-        x_raw.append(load_x(3))
+        x_raw.append(load_x(2))
+        load_planes(w1_scales, w1_planes_raw, range(5, 8))
         w1_raw.append(load_words(w1_words, 2, "w1_raw"))
-        nc.scalar.dma_start(
-            out=b2_rows[0 : 2 * BLOCKS * OUT_TILES, :],
-            in_=b2.rearrange("r n (m j) -> (r n m) j", j=P),
-        )
-        w2_planes = load_planes(w2_scales, "w2_planes")
-        w2_codes = [load_words(w2_words, 0, "w2_codes")]
+        x_raw.append(load_x(3))
         w1_raw.append(load_words(w1_words, 3, "w1_raw"))
-        for n in range(1, BLOCKS):
+        load_planes(w2_scales, w2_planes, range(0, 8))
+        w2_codes = []
+        for n in range(BLOCKS):
             w2_codes.append(load_words(w2_words, n, "w2_codes"))
 
         identity = keep.tile([P, P], BF16, name="identity")
         make_identity(nc, identity[:])
 
         ctx.enter_context(tc.manual_schedule())
-        w1_codes = []
-        x_mx = []
+        w1_codes = {}
+        x_mx = {}
+        x_grouped = []
+        for n in range(BLOCKS):
+            x_grouped.append(new_x_grouped(n))
 
         def x_step(n):
-            permuted, mx = prepare_x(n, x_grouped[n])
-            w1_codes.append(permuted)
-            x_mx.append(mx)
+            negate_x(n)
+            permute_w1(n)
+            quantise_x(n)
 
-        x_grouped = [group_x(0)]
+        turned = psum.tile([P, PACK + 1, P], BF16, name="bias_turned", tag="acc")
+        for t in range(PACK):
+            nc.tensor.transpose(
+                out=turned[:, t, :],
+                in_=bias_rows[:, 0:BS].rearrange("p (m t) -> p t m", t=PACK)[:, t, :],
+                identity=identity[:],
+            )
+        nc.tensor.transpose(
+            out=turned[:, PACK, :], in_=bias_rows[:, BS : BS + P], identity=identity[:]
+        )
+        b1_cols = keep.tile([P, 2 * BLOCKS, PACK], BF16, name="b1_cols")
+        nc.vector.tensor_copy(
+            out=b1_cols[:], in_=turned[:, 0:PACK, 0 : 2 * BLOCKS].rearrange("p t g -> p g t")
+        )
+        b2_cols = keep.tile([P, BLOCKS * OUT_TILES, 2], F32, name="b2_cols")
+        nc.vector.tensor_copy(
+            out=b2_cols[:],
+            in_=turned[:, PACK, 0 : 2 * BLOCKS * OUT_TILES].rearrange("p (r g) -> p g r", r=2),
+        )
+
+        group_x(0, 0)
+        group_x(0, 1)
         x_step(0)
-        x_grouped.append(group_x(1))
+        group_x(1, 0)
+        group_x(1, 1)
+        negate_x(1)
+        permute_w1(1)
 
         w1_planes = keep.tile([P, 2, BS], U8, name="w1_planes", align_bytes=64)
         for t in range(PACK):
@@ -277,17 +314,10 @@ def tile_scatteringmodule_pa_e_kernel(
                 in_=w1_planes_raw[:].rearrange("p r (m t) -> p r m t", t=PACK)[:, :, :, t],
             )
 
+        group_x(2, 0)
         hidden = {0: layer_1(0)}
-        x_step(1)
-        x_grouped.append(group_x(2))
-
-        b2_turned = psum.tile([P, P], BF16, name="b2_turned", tag="acc")
-        nc.tensor.transpose(out=b2_turned[:], in_=b2_rows[:], identity=identity[:])
-        b2_cols = keep.tile([P, BLOCKS * OUT_TILES, 2], F32, name="b2_cols")
-        nc.vector.tensor_copy(
-            out=b2_cols[:],
-            in_=b2_turned[:, 0 : 2 * BLOCKS * OUT_TILES].rearrange("p (r g) -> p g r", r=2),
-        )
+        quantise_x(1)
+        group_x(2, 1)
         x_step(2)
 
         h_mx = {0: new_h_mx()}
@@ -300,7 +330,8 @@ def tile_scatteringmodule_pa_e_kernel(
                 for u in range(len(RUNS)):
                     h_grouped.append(lay_h(n + 1, hidden[n + 1], u))
             if n == 0:
-                x_grouped.append(group_x(3))
+                group_x(3, 0)
+                group_x(3, 1)
             layer_2(n, h_mx[n])
             if n + 1 < BLOCKS:
                 h_mx[n + 1] = new_h_mx()

@@ -257,11 +257,11 @@ def tile_scatteringmodule_pa_e_kernel(
         x_raw.append(load_x(2))
         load_planes(w1_scales, w1_planes_raw, range(5, 8))
         w1_raw.append(load_words(w1_words, 2, "w1_raw"))
+        load_planes(w2_scales, w2_planes, range(0, 8))
+        w2_codes = [load_words(w2_words, 0, "w2_codes")]
         x_raw.append(load_x(3))
         w1_raw.append(load_words(w1_words, 3, "w1_raw"))
-        load_planes(w2_scales, w2_planes, range(0, 8))
-        w2_codes = []
-        for n in range(BLOCKS):
+        for n in range(1, BLOCKS):
             w2_codes.append(load_words(w2_words, n, "w2_codes"))
 
         identity = keep.tile([P, P], BF16, name="identity")
@@ -289,6 +289,15 @@ def tile_scatteringmodule_pa_e_kernel(
         nc.tensor.transpose(
             out=turned[:, PACK, :], in_=bias_rows[:, BS : BS + P], identity=identity[:]
         )
+
+        group_x(0, 0)
+        group_x(0, 1)
+        x_step(0)
+        group_x(1, 0)
+        group_x(1, 1)
+        negate_x(1)
+        permute_w1(1)
+
         b1_cols = keep.tile([P, 2 * BLOCKS, PACK], BF16, name="b1_cols")
         nc.vector.tensor_copy(
             out=b1_cols[:], in_=turned[:, 0:PACK, 0 : 2 * BLOCKS].rearrange("p t g -> p g t")
@@ -298,14 +307,6 @@ def tile_scatteringmodule_pa_e_kernel(
             out=b2_cols[:],
             in_=turned[:, PACK, 0 : 2 * BLOCKS * OUT_TILES].rearrange("p (r g) -> p g r", r=2),
         )
-
-        group_x(0, 0)
-        group_x(0, 1)
-        x_step(0)
-        group_x(1, 0)
-        group_x(1, 1)
-        negate_x(1)
-        permute_w1(1)
 
         w1_planes = keep.tile([P, 2, BS], U8, name="w1_planes", align_bytes=64)
         for t in range(PACK):

@@ -24,7 +24,7 @@ OUT_TILES = BS // P
 NEG_IM, RE, IM = 0, 1, 2
 RUNS = ((0, 256), (256, 128))
 MAX_QUANTIZE_WORDS = 1024
-X_ENGINES = ("SV", "SV", "SV", "SS")
+X_ENGINES = ("SV", "SV", "SV", "SV")
 H_ENGINES = ("SV", "SG", "SG", "SG")
 G_POSITIONS = 128
 
@@ -152,6 +152,17 @@ def tile_scatteringmodule_pa_e_kernel(
                     rhs_scale=moving[1][:, cols],
                     start=(w_part == 0),
                     stop=(w_part == 1),
+                )
+
+        def keep_warm(values):
+            sums = psum.tile([P, 512], F32, name="warm", tag="acc")
+            for first in range(0, values.shape[1], 512):
+                nc.tensor.matmul(
+                    out=sums[:],
+                    lhsT=identity[:],
+                    rhs=values[:, first : first + 512],
+                    start=True,
+                    stop=True,
                 )
 
         def layer_1(n):
@@ -297,6 +308,8 @@ def tile_scatteringmodule_pa_e_kernel(
         group_x(1, 1)
         negate_x(1)
         permute_w1(1)
+        keep_warm(x_grouped[1][:, IM].rearrange("p c t -> p (c t)"))
+        keep_warm(x_grouped[1][:, NEG_IM].rearrange("p c t -> p (c t)"))
 
         b1_cols = keep.tile([P, 2 * BLOCKS, PACK], BF16, name="b1_cols")
         nc.vector.tensor_copy(

@@ -12,6 +12,7 @@ FP8X4 = mybir.dt.float8_e4m3fn_x4
 ADD = mybir.AluOpType.add
 MULT = mybir.AluOpType.mult
 RELU = mybir.ActivationFunctionType.Relu
+COPY = mybir.ActivationFunctionType.Copy
 
 P = 128
 PACK = 4
@@ -26,6 +27,7 @@ RUNS = ((0, 256), (256, 128))
 MAX_QUANTIZE_WORDS = 1024
 X_ENGINES = ("SV", "SV", "SV", "SV")
 H_ENGINES = ("SV", "SG", "SG", "SG")
+NEG_ENGINES = "VVVS"
 G_POSITIONS = 128
 
 FLOPS = 2 * 8 * BLOCKS * POS * BS * BS
@@ -203,6 +205,13 @@ def tile_scatteringmodule_pa_e_kernel(
                             "p t (c i) -> p c t i", i=8
                         ),
                     )
+            if NEG_ENGINES[n] == "S":
+                nc.scalar.activation(
+                    out=grouped[:, NEG_IM].rearrange("p (c i) t -> p c t i", i=8),
+                    in_=hidden[:, 1, :, first : first + width].rearrange("p t (c i) -> p c t i", i=8),
+                    func=COPY,
+                    scale=-1.0,
+                )
             return grouped
 
         def new_h_mx():
@@ -210,9 +219,12 @@ def tile_scatteringmodule_pa_e_kernel(
             scales = work.tile([P, 3 * POS], U8, name="h_scales", align_bytes=64)
             return codes, scales
 
-        def quantise_h(grouped, u, mx):
+        def quantise_h(n, grouped, u, mx):
             first, width = RUNS[u]
-            nc.vector.tensor_scalar_mul(out=grouped[:, NEG_IM], in0=grouped[:, IM], scalar1=-1.0)
+            if NEG_ENGINES[n] == "V":
+                nc.vector.tensor_scalar_mul(
+                    out=grouped[:, NEG_IM], in0=grouped[:, IM], scalar1=-1.0
+                )
             quantise(
                 grouped[:].rearrange("p v c t -> p (v c t)"),
                 mx[0],
@@ -221,9 +233,17 @@ def tile_scatteringmodule_pa_e_kernel(
                 ((width, 2 * width), (0, width)),
             )
 
+        def store(result, n, m, b_from, b_to):
+            channel = n * BS + m * P
+            nc.sync.dma_start(
+                out=out_rows[b_from:b_to, channel : channel + P, :].rearrange("b c f -> c b f"),
+                in_=result[:].rearrange("p (b q) r -> p b (q r)", b=BATCH)[:, b_from:b_to, :],
+            )
+
         def layer_2(n, h_mx):
             for m in range(OUT_TILES):
                 result = results.tile([P, POS, 2], F32, name="result")
+                last = n == BLOCKS - 1 and m == OUT_TILES - 1
                 for u, (first, width) in enumerate(RUNS):
                     acc = psum.tile([P, 2, width], F32, name="acc_2_%d" % u, tag="acc")
                     mx_pair(
@@ -245,11 +265,12 @@ def tile_scatteringmodule_pa_e_kernel(
                         .to_broadcast([P, width, 2]),
                         op=ADD,
                     )
-                channel = n * BS + m * P
-                nc.sync.dma_start(
-                    out=out_rows[:, channel : channel + P, :].rearrange("b c f -> c b f"),
-                    in_=result[:].rearrange("p (b q) r -> p b (q r)", b=BATCH),
-                )
+                    if last and u == 0:
+                        store(result, n, m, 0, BATCH // 2)
+                if last:
+                    store(result, n, m, BATCH // 2, BATCH)
+                else:
+                    store(result, n, m, 0, BATCH)
 
         bias_rows = keep.tile([P, BS + P], BF16, name="bias_rows")
         nc.vector.memset(bias_rows[:], 0.0)
@@ -305,28 +326,26 @@ def tile_scatteringmodule_pa_e_kernel(
         group_x(0, 1)
         x_step(0)
         group_x(1, 0)
+        b1_cols = keep.tile([P, 2 * BLOCKS, PACK], BF16, name="b1_cols")
+        nc.scalar.copy(
+            out=b1_cols[:], in_=turned[:, 0:PACK, 0 : 2 * BLOCKS].rearrange("p t g -> p g t")
+        )
+        b2_cols = keep.tile([P, BLOCKS * OUT_TILES, 2], F32, name="b2_cols")
+        nc.scalar.copy(
+            out=b2_cols[:],
+            in_=turned[:, PACK, 0 : 2 * BLOCKS * OUT_TILES].rearrange("p (r g) -> p g r", r=2),
+        )
         group_x(1, 1)
         negate_x(1)
         permute_w1(1)
         keep_warm(x_grouped[1][:, IM].rearrange("p c t -> p (c t)"))
         keep_warm(x_grouped[1][:, NEG_IM].rearrange("p c t -> p (c t)"))
 
-        b1_cols = keep.tile([P, 2 * BLOCKS, PACK], BF16, name="b1_cols")
-        nc.vector.tensor_copy(
-            out=b1_cols[:], in_=turned[:, 0:PACK, 0 : 2 * BLOCKS].rearrange("p t g -> p g t")
-        )
-        b2_cols = keep.tile([P, BLOCKS * OUT_TILES, 2], F32, name="b2_cols")
-        nc.vector.tensor_copy(
-            out=b2_cols[:],
-            in_=turned[:, PACK, 0 : 2 * BLOCKS * OUT_TILES].rearrange("p (r g) -> p g r", r=2),
-        )
-
         w1_planes = keep.tile([P, 2, BS], U8, name="w1_planes", align_bytes=64)
-        for t in range(PACK):
-            nc.vector.tensor_copy(
-                out=w1_planes[:, :, t * P : (t + 1) * P],
-                in_=w1_planes_raw[:].rearrange("p r (m t) -> p r m t", t=PACK)[:, :, :, t],
-            )
+        nc.vector.tensor_copy(
+            out=w1_planes[:].rearrange("p r (t m i) -> p r m t i", t=PACK, i=16),
+            in_=w1_planes_raw[:].rearrange("p r (m i t) -> p r m t i", t=PACK, i=16),
+        )
 
         group_x(2, 0)
         hidden = {0: layer_1(0)}
@@ -336,7 +355,7 @@ def tile_scatteringmodule_pa_e_kernel(
 
         h_mx = {0: new_h_mx()}
         for u in range(len(RUNS)):
-            quantise_h(lay_h(0, hidden[0], u), u, h_mx[0])
+            quantise_h(0, lay_h(0, hidden[0], u), u, h_mx[0])
         hidden[1] = layer_1(1)
         for n in range(BLOCKS):
             if n + 1 < BLOCKS:
@@ -350,7 +369,7 @@ def tile_scatteringmodule_pa_e_kernel(
             if n + 1 < BLOCKS:
                 h_mx[n + 1] = new_h_mx()
                 for u in range(len(RUNS)):
-                    quantise_h(h_grouped[u], u, h_mx[n + 1])
+                    quantise_h(n + 1, h_grouped[u], u, h_mx[n + 1])
             if n == 0:
                 x_step(3)
             if n + 2 < BLOCKS:

@@ -374,3 +374,6 @@ def tile_scatteringmodule_pa_e_kernel(
                 x_step(3)
             if n + 2 < BLOCKS:
                 hidden[n + 2] = layer_1(n + 2)
+            if n + 1 == BLOCKS - 1:
+                for u in range(len(RUNS)):
+                    keep_warm(h_grouped[u][:, NEG_IM].rearrange("p c t -> p (c t)"))

@@ -54,8 +54,8 @@ def tile_scatteringmodule_pa_e_kernel(
 
     with ExitStack() as ctx:
         keep = ctx.enter_context(tc.tile_pool(name="keep", bufs=1))
-        work = ctx.enter_context(tc.tile_pool(name="work", bufs=2))
-        results = ctx.enter_context(tc.tile_pool(name="results", bufs=4))
+        work = ctx.enter_context(tc.tile_pool(name="work", bufs=3))
+        results = ctx.enter_context(tc.tile_pool(name="results", bufs=8))
         psum = ctx.enter_context(tc.psum_pool(name="psum", bufs=8))
 
         def load_x(n):
@@ -129,8 +129,8 @@ def tile_scatteringmodule_pa_e_kernel(
         def permute_w1(n):
             permuted = keep.tile([P, 2, BS], U32, name="w1_codes%d" % n, align_bytes=64)
             nc.vector.tensor_copy(
-                out=permuted[:].bitcast(I32).rearrange("p r (t m i) -> p r m t i", t=PACK, i=4),
-                in_=w1_raw[n][:].bitcast(I32).rearrange("p r (m i t) -> p r m t i", t=PACK, i=4),
+                out=permuted[:].bitcast(I32).rearrange("p r (t m) -> p r m t", t=PACK),
+                in_=w1_raw[n][:].bitcast(I32).rearrange("p r (m t) -> p r m t", t=PACK),
             )
             w1_codes[n] = permuted
 

from contextlib import ExitStack

import concourse.mybir as mybir
from concourse.masks import make_identity

F32 = mybir.dt.float32
BF16 = mybir.dt.bfloat16
I32 = mybir.dt.int32
U32 = mybir.dt.uint32
U8 = mybir.dt.uint8
FP8X4 = mybir.dt.float8_e4m3fn_x4
ADD = mybir.AluOpType.add
MULT = mybir.AluOpType.mult
RELU = mybir.ActivationFunctionType.Relu
COPY = mybir.ActivationFunctionType.Copy

P = 128
PACK = 4
BATCH = 4
SPOTS = 96
POS = BATCH * SPOTS
BLOCKS = 4
BS = 512
OUT_TILES = BS // P
NEG_IM, RE, IM = 0, 1, 2
RUNS = ((0, 256), (256, 128))
MAX_QUANTIZE_WORDS = 1024
X_ENGINES = ("SV", "SV", "SV", "SV")
H_ENGINES = ("SV", "SG", "SG", "SG")
NEG_ENGINES = "VVVS"
G_POSITIONS = 128

FLOPS = 2 * 8 * BLOCKS * POS * BS * BS


def powers_of_two(columns):
    cuts = []
    width = MAX_QUANTIZE_WORDS
    while columns > 0:
        if width <= columns:
            cuts.append(width)
            columns -= width
        else:
            width //= 2
    return cuts


def tile_scatteringmodule_pa_e_kernel(
    tc, xh, w1_words, w1_scales, w2_words, w2_scales, b1, b2, out
):
    nc = tc.nc
    x_rows = xh.rearrange("b c o h w r -> b c (o h w r)")
    out_rows = out.rearrange("b c o h w r -> b c (o h w r)")

    with ExitStack() as ctx:
        keep = ctx.enter_context(tc.tile_pool(name="keep", bufs=1))
        work = ctx.enter_context(tc.tile_pool(name="work", bufs=3))
        results = ctx.enter_context(tc.tile_pool(name="results", bufs=8))
        psum = ctx.enter_context(tc.psum_pool(name="psum", bufs=8))

        def load_x(n):
            raw = keep.tile([P, BATCH, PACK * SPOTS * 2], BF16, name="x_raw%d" % n)
            rows = x_rows[:, n * BS : (n + 1) * BS, :]
            nc.sync.dma_start(out=raw[:], in_=rows.rearrange("b (p t) f -> p b (t f)", t=PACK))
            return raw

        def load_words(words, n, name):
            codes = keep.tile([P, 2, BS], U32, name="%s%d" % (name, n), align_bytes=64)
            by_word = words.rearrange("g p n t -> p g (n t)").bitcast(I32)
            by_part = by_word.rearrange("p (r m) w -> p r m w", r=2)
            nc.sync.dma_start(out=codes[:].bitcast(I32), in_=by_part[:, :, n, :])
            return codes

        def new_planes(name):
            planes = keep.tile([P, 2, BS], U8, name=name, align_bytes=64)
            nc.vector.memset(planes[:].bitcast(I32), 0)
            return planes

        def load_planes(scales, planes, pieces):
            for piece in pieces:
                quad, part = divmod(piece, 2)
                nc.sync.dma_start(
                    out=planes[32 * quad : 32 * quad + 16, part, :].bitcast(I32),
                    in_=scales[
                        part * BLOCKS : (part + 1) * BLOCKS, 4 * quad : 4 * quad + 4, :
                    ].bitcast(I32),
                )

        def lay_side_by_side(engine, target, source):
            if engine == "S":
                nc.scalar.copy(out=target, in_=source)
            elif engine == "V":
                nc.vector.tensor_copy(out=target, in_=source)
            else:
                for g in range(0, target.shape[1], G_POSITIONS):
                    nc.gpsimd.tensor_scalar(
                        out=target[:, g : g + G_POSITIONS],
                        in0=source[:, g : g + G_POSITIONS],
                        scalar1=1.0,
                        scalar2=0.0,
                        op0=MULT,
                        op1=ADD,
                    )

        def quantise(flat, codes, scales, first, spans):
            for start, columns in spans:
                for cut in powers_of_two(columns):
                    nc.vector.quantize_mx(
                        out=codes[:, first + start : first + start + cut].bitcast(FP8X4),
                        scales=scales[:, first + start : first + start + cut],
                        in_=flat[:, PACK * start : PACK * (start + cut)],
                    )
                    start += cut

        def new_x_grouped(n):
            return keep.tile([P, 3, POS, PACK], BF16, name="x_grouped%d" % n, align_bytes=64)

        def group_x(n, part):
            raw = x_raw[n][:].rearrange(
                "p b (t c i r) -> p r b c t i", t=PACK, c=SPOTS // 4, i=4, r=2
            )
            by_batch = x_grouped[n][:].rearrange("p v (b c i) t -> p v b c t i", b=BATCH, i=4)
            lay_side_by_side(X_ENGINES[n][part], by_batch[:, (RE, IM)[part]], raw[:, part])

        def negate_x(n):
            grouped = x_grouped[n]
            nc.vector.tensor_scalar_mul(out=grouped[:, NEG_IM], in0=grouped[:, IM], scalar1=-1.0)

        def permute_w1(n):
            permuted = keep.tile([P, 2, BS], U32, name="w1_codes%d" % n, align_bytes=64)
            nc.vector.tensor_copy(
                out=permuted[:].bitcast(I32).rearrange("p r (t m) -> p r m t", t=PACK),
                in_=w1_raw[n][:].bitcast(I32).rearrange("p r (m t) -> p r m t", t=PACK),
            )
            w1_codes[n] = permuted

        def quantise_x(n):
            codes = keep.tile([P, 3 * POS], U32, name="x_codes%d" % n, align_bytes=64)
            scales = keep.tile([P, 3 * POS], U8, name="x_scales%d" % n, align_bytes=64)
            quantise(
                x_grouped[n][:].rearrange("p v c t -> p (v c t)"), codes, scales, 0, ((0, 3 * POS),)
            )
            x_mx[n] = (codes, scales)

        def mx_pair(acc, codes, planes, n, tile_index, moving, re_im, neg_re, columns):
            cols_w = slice(tile_index * P, (tile_index + 1) * P)
            for w_part, start in ((0, re_im), (1, neg_re)):
                cols = slice(start, start + columns)
                nc.tensor.matmul_mx(
                    out=acc,
                    lhsT=codes[:, w_part, cols_w].bitcast(FP8X4),
                    lhsT_scale=planes[4 * n : P, w_part, cols_w],
                    rhs=moving[0][:, cols].bitcast(FP8X4),
                    rhs_scale=moving[1][:, cols],
                    start=(w_part == 0),
                    stop=(w_part == 1),
                )

        def keep_warm(values):
            sums = psum.tile([P, 512], F32, name="warm", tag="acc")
            for first in range(0, values.shape[1], 512):
                nc.tensor.matmul(
                    out=sums[:],
                    lhsT=identity[:],
                    rhs=values[:, first : first + 512],
                    start=True,
                    stop=True,
                )

        def layer_1(n):
            hidden = work.tile([P, 2, PACK, POS], BF16, name="h_planar")
            for t in range(PACK):
                wide = psum.tile([P, 512], F32, name="acc_1_wide", tag="acc")
                mx_pair(wide[:], w1_codes[n], w1_planes, n, t, x_mx[n], POS, 0, 512)
                narrow = psum.tile([P, 256], F32, name="acc_1_narrow", tag="acc")
                mx_pair(narrow[:], w1_codes[n], w1_planes, n, t, x_mx[n], POS + 512, 512, 256)
                for part, target, source in (
                    (0, hidden[:, 0, t, :], wide[:, 0:POS]),
                    (1, hidden[:, 1, t, 0 : 512 - POS], wide[:, POS:512]),
                    (1, hidden[:, 1, t, 512 - POS : POS], narrow[:]),
                ):
                    nc.scalar.activation(
                        out=target,
                        in_=source,
                        func=RELU,
                        bias=b1_cols[:, part * BLOCKS + n, t : t + 1],
                    )
            return hidden

        def lay_h(n, hidden, u):
            first, width = RUNS[u]
            grouped = work.tile([P, 3, width, PACK], BF16, name="h_grouped%d" % u, align_bytes=64)
            for part, variant in ((0, RE), (1, IM)):
                if H_ENGINES[n][part] == "G":
                    lay_side_by_side(
                        "G",
                        grouped[:, variant],
                        hidden[:, part, :, first : first + width].rearrange("p t c -> p c t"),
                    )
                else:
                    lay_side_by_side(
                        H_ENGINES[n][part],
                        grouped[:, variant].rearrange("p (c i) t -> p c t i", i=8),
                        hidden[:, part, :, first : first + width].rearrange(
                            "p t (c i) -> p c t i", i=8
                        ),
                    )
            if NEG_ENGINES[n] == "S":
                nc.scalar.activation(
                    out=grouped[:, NEG_IM].rearrange("p (c i) t -> p c t i", i=8),
                    in_=hidden[:, 1, :, first : first + width].rearrange("p t (c i) -> p c t i", i=8),
                    func=COPY,
                    scale=-1.0,
                )
            return grouped

        def new_h_mx():
            codes = work.tile([P, 3 * POS], U32, name="h_codes", align_bytes=64)
            scales = work.tile([P, 3 * POS], U8, name="h_scales", align_bytes=64)
            return codes, scales

        def quantise_h(n, grouped, u, mx):
            first, width = RUNS[u]
            if NEG_ENGINES[n] == "V":
                nc.vector.tensor_scalar_mul(
                    out=grouped[:, NEG_IM], in0=grouped[:, IM], scalar1=-1.0
                )
            quantise(
                grouped[:].rearrange("p v c t -> p (v c t)"),
                mx[0],
                mx[1],
                3 * first,
                ((width, 2 * width), (0, width)),
            )

        def store(result, n, m, b_from, b_to):
            channel = n * BS + m * P
            nc.sync.dma_start(
                out=out_rows[b_from:b_to, channel : channel + P, :].rearrange("b c f -> c b f"),
                in_=result[:].rearrange("p (b q) r -> p b (q r)", b=BATCH)[:, b_from:b_to, :],
            )

        def layer_2(n, h_mx):
            for m in range(OUT_TILES):
                result = results.tile([P, POS, 2], F32, name="result")
                last = n == BLOCKS - 1 and m == OUT_TILES - 1
                for u, (first, width) in enumerate(RUNS):
                    acc = psum.tile([P, 2, width], F32, name="acc_2_%d" % u, tag="acc")
                    mx_pair(
                        acc[:].rearrange("p r c -> p (r c)"),
                        w2_codes[n],
                        w2_planes,
                        n,
                        m,
                        h_mx,
                        3 * first + width,
                        3 * first,
                        2 * width,
                    )
                    nc.vector.tensor_tensor(
                        out=result[:, first : first + width, :],
                        in0=acc[:].rearrange("p r c -> p c r"),
                        in1=b2_cols[:, n * OUT_TILES + m, :]
                        .unsqueeze(1)
                        .to_broadcast([P, width, 2]),
                        op=ADD,
                    )
                    if last and u == 0:
                        store(result, n, m, 0, BATCH // 2)
                if last:
                    store(result, n, m, BATCH // 2, BATCH)
                else:
                    store(result, n, m, 0, BATCH)

        bias_rows = keep.tile([P, BS + P], BF16, name="bias_rows")
        nc.vector.memset(bias_rows[:], 0.0)
        nc.scalar.dma_start(out=bias_rows[0 : 2 * BLOCKS, 0:BS], in_=b1.rearrange("r n c -> (r n) c"))
        nc.scalar.dma_start(
            out=bias_rows[0 : 2 * BLOCKS * OUT_TILES, BS : BS + P],
            in_=b2.rearrange("r n (m j) -> (r n m) j", j=P),
        )
        w1_planes_raw = new_planes("w1_planes_raw")
        w2_planes = new_planes("w2_planes")
        x_raw = [load_x(0)]
        w1_raw = [load_words(w1_words, 0, "w1_raw")]
        x_raw.append(load_x(1))
        load_planes(w1_scales, w1_planes_raw, range(0, 5))
        w1_raw.append(load_words(w1_words, 1, "w1_raw"))
        x_raw.append(load_x(2))
        load_planes(w1_scales, w1_planes_raw, range(5, 8))
        w1_raw.append(load_words(w1_words, 2, "w1_raw"))
        load_planes(w2_scales, w2_planes, range(0, 8))
        w2_codes = [load_words(w2_words, 0, "w2_codes")]
        x_raw.append(load_x(3))
        w1_raw.append(load_words(w1_words, 3, "w1_raw"))
        for n in range(1, BLOCKS):
            w2_codes.append(load_words(w2_words, n, "w2_codes"))

        identity = keep.tile([P, P], BF16, name="identity")
        make_identity(nc, identity[:])

        ctx.enter_context(tc.manual_schedule())
        w1_codes = {}
        x_mx = {}
        x_grouped = []
        for n in range(BLOCKS):
            x_grouped.append(new_x_grouped(n))

        def x_step(n):
            negate_x(n)
            permute_w1(n)
            quantise_x(n)

        turned = psum.tile([P, PACK + 1, P], BF16, name="bias_turned", tag="acc")
        for t in range(PACK):
            nc.tensor.transpose(
                out=turned[:, t, :],
                in_=bias_rows[:, 0:BS].rearrange("p (m t) -> p t m", t=PACK)[:, t, :],
                identity=identity[:],
            )
        nc.tensor.transpose(
            out=turned[:, PACK, :], in_=bias_rows[:, BS : BS + P], identity=identity[:]
        )

        group_x(0, 0)
        group_x(0, 1)
        x_step(0)
        group_x(1, 0)
        b1_cols = keep.tile([P, 2 * BLOCKS, PACK], BF16, name="b1_cols")
        nc.scalar.copy(
            out=b1_cols[:], in_=turned[:, 0:PACK, 0 : 2 * BLOCKS].rearrange("p t g -> p g t")
        )
        b2_cols = keep.tile([P, BLOCKS * OUT_TILES, 2], F32, name="b2_cols")
        nc.scalar.copy(
            out=b2_cols[:],
            in_=turned[:, PACK, 0 : 2 * BLOCKS * OUT_TILES].rearrange("p (r g) -> p g r", r=2),
        )
        group_x(1, 1)
        negate_x(1)
        permute_w1(1)
        keep_warm(x_grouped[1][:, IM].rearrange("p c t -> p (c t)"))
        keep_warm(x_grouped[1][:, NEG_IM].rearrange("p c t -> p (c t)"))

        w1_planes = keep.tile([P, 2, BS], U8, name="w1_planes", align_bytes=64)
        nc.vector.tensor_copy(
            out=w1_planes[:].rearrange("p r (t m i) -> p r m t i", t=PACK, i=16),
            in_=w1_planes_raw[:].rearrange("p r (m i t) -> p r m t i", t=PACK, i=16),
        )

        group_x(2, 0)
        hidden = {0: layer_1(0)}
        quantise_x(1)
        group_x(2, 1)
        x_step(2)

        h_mx = {0: new_h_mx()}
        for u in range(len(RUNS)):
            quantise_h(0, lay_h(0, hidden[0], u), u, h_mx[0])
        hidden[1] = layer_1(1)
        for n in range(BLOCKS):
            if n + 1 < BLOCKS:
                h_grouped = []
                for u in range(len(RUNS)):
                    h_grouped.append(lay_h(n + 1, hidden[n + 1], u))
            if n == 0:
                group_x(3, 0)
                group_x(3, 1)
            layer_2(n, h_mx[n])
            if n + 1 < BLOCKS:
                h_mx[n + 1] = new_h_mx()
                for u in range(len(RUNS)):
                    quantise_h(n + 1, h_grouped[u], u, h_mx[n + 1])
            if n == 0:
                x_step(3)
            if n + 2 < BLOCKS:
                hidden[n + 2] = layer_1(n + 2)
            if n + 1 == BLOCKS - 1:
                for u in range(len(RUNS)):
                    keep_warm(h_grouped[u][:, NEG_IM].rearrange("p c t -> p (c t)"))
